import numpy as np
import ml_dtypes


def mxq(x, axis, fmt="e4m3"):
    dtype, down = {"e4m3": (ml_dtypes.float8_e4m3fn, 7), "e5m2": (ml_dtypes.float8_e5m2, 14)}[fmt]
    v = np.moveaxis(np.asarray(x, np.float32).astype(ml_dtypes.bfloat16).astype(np.float64), axis, -1)
    blocks = v.reshape(v.shape[:-1] + (-1, 32))
    amax = np.abs(blocks).max(-1, keepdims=True)
    byte = np.maximum(np.where(amax > 0, np.frexp(amax)[1] - 1 + 127, 0) - down, 1)
    scale = np.exp2(byte - 127.0)
    codes = (blocks / scale).astype(np.float32).astype(dtype).astype(np.float64)
    return np.moveaxis((codes * scale).reshape(v.shape), -1, axis)


WIDE = False


def mx_kscale(k):
    if not WIDE:
        return np.ones(k)
    levels = np.array([18, -18])
    if k % 512:
        return np.exp2(np.random.permutation(np.resize(levels, k // 32))).repeat(32)
    a = np.empty((k // 512, 16))
    for p in range(k // 512):
        a[p, :8] = np.random.permutation(np.resize(levels, 8))
        for g in range(8):
            far = levels[np.abs(levels - a[p, g]) >= 10]
            a[p, g + 8] = far[np.random.randint(len(far))]
    return np.exp2(a.ravel()).repeat(32)


BF16 = ml_dtypes.bfloat16


def bf(x):
    return np.asarray(x, np.float32).astype(BF16)


def f64(x):
    return np.asarray(x).astype(np.float64)


B, N, D, H, DH = 2, 512, 1024, 2, 512
E = H * DH
K_POLY = 3
SIG = 2.0


def setup_inputs():
    u = mx_kscale(N)
    v = mx_kscale(E)
    s = mx_kscale(B * N).reshape(B, N)
    fu = u / np.min(u)
    fs = s / np.max(s)
    g = np.random.standard_normal
    lg = g((B, H, N, N)) * SIG
    e = np.exp(lg - lg.max(-1, keepdims=True))
    x0 = bf(g((B, N, D)))
    att0 = bf(e / e.sum(-1, keepdims=True))
    Wv0 = bf(g((D, E)) * 1.5 / np.sqrt(D))
    bv = bf(g(E) * 0.2)
    w0 = bf(0.25 + 0.05 * g(H))
    w1 = bf(1.0 + 0.1 * g(H))
    wK = bf(0.2 + 0.03 * g(H))
    att2 = f64(att0) @ f64(att0)
    go = bf(g((B, N, E)) * np.exp2(np.random.randint(-6, 1, (B, N, 1))) * 2.0 / fu[None, :, None] * v * np.min(s))
    return {
        "x": bf(f64(x0) * fs[:, :, None]),
        "att": bf(f64(att0) * fu[None, None, :, None] / fs[:, None, None, :]),
        "Wv": bf(f64(Wv0) / v),
        "bv": bv,
        "w0": w0,
        "w1": w1,
        "wK": wK,
        "att2": np.asarray(att2, np.float32),
        "grad_out": go,
    }


def reference(x, att, Wv, bv, w0, w1, wK, att2, grad_out):
    a = f64(att)
    attK = a + (K_POLY - 1) * (f64(att2) - a)
    c0 = f64(w0)[None, :, None, None]
    c1 = f64(w1)[None, :, None, None]
    cK = f64(wK)[None, :, None, None]
    gf = c0 * np.eye(N)[None, None] + c1 * a + cK * attK
    do = f64(grad_out).reshape(B, N, H, DH).transpose(0, 2, 1, 3)
    dv = mxq(gf, 2, "e4m3").transpose(0, 1, 3, 2) @ mxq(do, 2, "e5m2")
    dvv = dv.transpose(0, 2, 1, 3).reshape(B * N, E)
    dx = mxq(dvv, 1, "e5m2") @ mxq(f64(Wv), 1, "e4m3").T
    dWv = mxq(f64(x).reshape(B * N, D), 0, "e4m3").T @ mxq(dvv, 0, "e5m2")
    return dx.reshape(B, N, D), dWv

@@ -1,0 +1,524 @@
+from contextlib import ExitStack
+
+import concourse.mybir as mybir
+from concourse.masks import make_identity
+
+B, H, N, D, E = 2, 2, 512, 1024, 1024
+DH = 512
+P = 128
+PACK = 4
+F32 = mybir.dt.float32
+BF16 = mybir.dt.bfloat16
+U32 = mybir.dt.uint32
+U8 = mybir.dt.uint8
+E4M3 = mybir.dt.float8_e4m3fn_x4
+E5M2 = mybir.dt.float8_e5m2_x4
+ALU = mybir.AluOpType
+
+FLOPS = 2 * (B * H * N * N * DH) + 2 * 2 * (B * N * E * D)
+
+
+def tile_gfsa_pa_v_kernel(tc, x, att, Wv, bv, w0, w1, wK, att2, grad_out, out_0, out_1):
+    nc = tc.nc
+    with ExitStack() as ctx:
+        const = ctx.enter_context(tc.tile_pool(name="const", bufs=1))
+        raw = ctx.enter_context(tc.tile_pool(name="raw", bufs=1))
+        stage = ctx.enter_context(tc.tile_pool(name="stage", bufs=2))
+        keep = ctx.enter_context(tc.tile_pool(name="keep", bufs=1))
+        outs = ctx.enter_context(tc.tile_pool(name="outs", bufs=6))
+        pst = ctx.enter_context(tc.psum_pool(name="pst", bufs=2))
+        psm = ctx.enter_context(tc.psum_pool(name="psm", bufs=6))
+        ctx.enter_context(tc.manual_schedule())
+
+        wt = {}
+        for nm, src in (("w0", w0), ("w1", w1), ("wK", wK)):
+            t = const.tile([P, H], BF16, name="wt_" + nm)
+            nc.scalar.dma_start(out=t[:], in_=src.partition_broadcast(P))
+            wt[nm] = t
+
+        do_raw = {}
+        att_sb = {}
+        att2_sb = {}
+        x_raw = {}
+
+        def load_do(b, h):
+            t = raw.tile([P, PACK, DH], BF16, name="do_raw%d%d" % (b, h))
+            nc.sync.dma_start(out=t[:], in_=grad_out[b, :, DH * h : DH * (h + 1)].rearrange("(p j) e -> p j e", j=PACK))
+            do_raw[b, h] = t
+
+        def load_att(b, h):
+            t = raw.tile([P, PACK, N], BF16, name="att_sb", bufs=3)
+            nc.sync.dma_start(out=t[:], in_=att[b, h].rearrange("(p j) k -> p j k", j=PACK))
+            att_sb[b, h] = t
+
+        def load_att2(b, h):
+            t = raw.tile([P, PACK, N], F32, name="att2_sb", bufs=3)
+            nc.sync.dma_start(out=t[:], in_=att2[b, h].rearrange("(p j) k -> p j k", j=PACK))
+            att2_sb[b, h] = t
+
+        def load_x(b):
+            t = raw.tile([P, PACK, D], BF16, name="x_raw%d" % b)
+            nc.sync.dma_start(out=t[:], in_=x[b].rearrange("(p j) d -> p j d", j=PACK))
+            x_raw[b] = t
+
+        wv_raw = {}
+
+        def load_wv(i0):
+            t = raw.tile([P, 4, E], BF16, name="wv_raw%d" % i0)
+            nc.sync.dma_start(out=t[:], in_=Wv[512 * i0 : 512 * (i0 + 1), :].rearrange("(i p) e -> p i e", p=P))
+            wv_raw[i0] = t
+
+        id_bf = const.tile([P, P], BF16)
+        make_identity(nc, id_bf[:])
+        id_f = const.tile([P, P], F32)
+        make_identity(nc, id_f[:])
+        irep = const.tile([P, PACK, P], BF16)
+        for j in range(PACK):
+            nc.vector.tensor_copy(out=irep[:, j, :], in_=id_bf[:])
+        diag = {}
+        for h in range(H):
+            for nm, sgn in (("w1", 1.0), ("wK", -1.0), ("w0", 1.0)):
+                t = const.tile([P, P], BF16, name="diag_%s%d" % (nm, h))
+                nc.vector.tensor_scalar(out=t[:], in0=id_bf[:], scalar1=wt[nm][:, h : h + 1], scalar2=sgn, op0=ALU.mult, op1=ALU.mult)
+                diag[nm, h] = t
+        wk2 = const.tile([P, H], F32)
+        nc.vector.tensor_scalar(out=wk2[:], in0=wt["wK"][:], scalar1=2.0, scalar2=None, op0=ALU.mult)
+        c1 = const.tile([P, H], F32)
+        nc.vector.tensor_tensor(out=c1[:], in0=wt["w1"][:], in1=wt["wK"][:], op=ALU.subtract)
+        w0f = const.tile([P, H], F32)
+        nc.vector.tensor_copy(out=w0f[:], in_=wt["w0"][:])
+        KD = 256
+        dmask = const.tile([P, PACK * (KD + 1)], F32)
+        nc.gpsimd.memset(dmask[:], 0.0)
+        nc.gpsimd.tensor_scalar(
+            out=dmask[:].rearrange("p (j x) -> p j x", x=KD + 1)[:, :, 0:KD:PACK],
+            in0=irep[:, :, 0 : KD // PACK],
+            scalar1=w0f[:, 0:1],
+            scalar2=0.0,
+            op0=ALU.mult,
+            op1=ALU.add,
+        )
+
+        def codes_tile(name, bufs=1):
+            c = keep.tile([P, 512], U32, name=name + "_c", align_bytes=64, bufs=bufs)
+            s = keep.tile([P, 512], U8, name=name + "_s", align_bytes=64, bufs=bufs)
+            return c, s
+
+        def quant(cs, src, fmt):
+            c, s = cs
+            nc.vector.quantize_mx(out=c[:].bitcast(fmt), scales=s[:], in_=src[:])
+
+        do_g, do_q, gf_g, gf_q, f_sb, g_g, g_q, t_g, t_q = {}, {}, {}, {}, {}, {}, {}, {}, {}
+        wv_g, wv_q, x_g, x_q = {}, {}, {}, {}
+
+        def copy(eng, out, in_):
+            if eng == "v":
+                nc.vector.tensor_copy(out=out, in_=in_)
+            else:
+                nc.scalar.copy(out=out, in_=in_)
+
+        def do_int(b, h, eng):
+            t = stage.tile([P, 2048], BF16, name="do_g", align_bytes=64)
+            copy(eng, t[:].rearrange("p (t m j) -> p t m j", t=PACK, j=PACK),
+                 do_raw[b, h][:].rearrange("p j (m t) -> p t m j", t=PACK))
+            do_g[b, h] = t
+
+        def do_quant(b, h):
+            do_q[b, h] = codes_tile("do_q", 2)
+            quant(do_q[b, h], do_g[b, h], E5M2)
+
+        lin00 = stage.tile([P, PACK, KD], F32, name="lin00", bufs=1)
+
+        def gf_lin():
+            nc.vector.scalar_tensor_tensor(
+                out=lin00[:],
+                in0=att_sb[0, 0][:, :, 0:KD],
+                scalar=c1[:, 0:1],
+                in1=dmask[:, 0 : PACK * KD].rearrange("p (j k) -> p j k", j=PACK),
+                op0=ALU.mult,
+                op1=ALU.add,
+            )
+
+        lins = {}
+
+        def gf_pe(b, h, kb):
+            ks = slice(P * kb, P * (kb + 1))
+            if (b, h) == (0, 0) and kb < KD // P:
+                lins[b, h, kb] = lin00[:, :, ks].rearrange("p j k -> p k j")
+            else:
+                bank = psm.tile([P, 512], F32, name="mm")
+                bj = bank[:].rearrange("p (j k) -> p j k", j=PACK)
+                rhs = att_sb[b, h][:, :, ks]
+                nc.tensor.matmul(out=bj, lhsT=diag["w1", h][:], rhs=rhs, start=True, stop=False)
+                ms = slice(32 * kb, 32 * (kb + 1))
+                nc.tensor.matmul(
+                    out=bank[:, 0:387].rearrange("p (j x) -> p j x", x=129)[:, :, 0:125:4],
+                    lhsT=diag["w0", h][:], rhs=irep[:, 0:3, ms], start=False, stop=False)
+                nc.tensor.matmul(out=bank[:, 387:512:4], lhsT=diag["w0", h][:], rhs=irep[:, 3, ms], start=False, stop=False)
+                nc.tensor.matmul(out=bj, lhsT=diag["wK", h][:], rhs=rhs, start=False, stop=True)
+                lins[b, h, kb] = bj.rearrange("p j k -> p k j")
+
+        def gf_sum(b, h, kb):
+            if kb == 0:
+                gf_g[b, h] = stage.tile([P, 2048], BF16, name="gf_g", align_bytes=64)
+            ks = slice(P * kb, P * (kb + 1))
+            nc.vector.scalar_tensor_tensor(
+                out=gf_g[b, h][:, 512 * kb : 512 * (kb + 1)].rearrange("p (k j) -> p k j", j=PACK),
+                in0=att2_sb[b, h][:, :, ks].rearrange("p j k -> p k j"),
+                scalar=wk2[:, h : h + 1],
+                in1=lins[b, h, kb],
+                op0=ALU.mult,
+                op1=ALU.add,
+            )
+
+        def gf_quant(b, h):
+            gf_q[b, h] = codes_tile("gf_q", 2)
+            quant(gf_q[b, h], gf_g[b, h], E4M3)
+
+        def mx(out, l, ls, lf, r, rs, rf, cols_l, cols_r, start, stop):
+            nc.tensor.matmul_mx(
+                out=out, lhsT=l[:, cols_l].bitcast(lf), lhsT_scale=ls[:, cols_l],
+                rhs=r[:, cols_r].bitcast(rf), rhs_scale=rs[:, cols_r], start=start, stop=stop)
+
+        banks = {}
+
+        def mm_bank(*k):
+            bank = psm.tile([P, 512], F32, name="mm")
+            banks[k] = bank
+            return bank
+
+        def feat_mm(b, h, t):
+            bank = mm_bank("f", b, h, t)
+            mx(bank[:], do_q[b, h][0], do_q[b, h][1], E5M2, gf_q[b, h][0], gf_q[b, h][1], E4M3,
+               slice(P * t, P * (t + 1)), slice(0, 512), True, True)
+
+        def feat_out(b, h, t, eng):
+            if t == 0:
+                f_sb[b, h] = stage.tile([P, PACK, 2, 256], BF16, name="f_sb", align_bytes=64)
+            copy(eng, f_sb[b, h][:, t].rearrange("p u (q e) -> p u q e", e=2),
+                 banks["f", b, h, t][:].rearrange("p (q u e) -> p u q e", u=2, e=2))
+
+        def turn(b, h, tt):
+            bank = pst.tile([P, 2, 2, P], F32, name="tr")
+            banks["t", b, h, tt] = bank
+            for t2 in range(2):
+                words = f_sb[b, h][:, 2 * tt + t2].rearrange("p u w -> p (u w)").bitcast(F32)
+                for u in range(2):
+                    nc.tensor.transpose(bank[:, t2, u, :], words[:, P * u : P * (u + 1)], id_f[:])
+
+        def turn_out(b, h, tt, eng):
+            if tt == 0:
+                t_g[b, h] = stage.tile([P, 2048], BF16, name="t_g", align_bytes=64)
+            copy(eng, t_g[b, h][:, 1024 * tt : 1024 * (tt + 1)].bitcast(F32).rearrange("p (t r u) -> p t r u", t=2, u=2),
+                 banks["t", b, h, tt][:].rearrange("p t u r -> p t r u"))
+
+        def g_int(b, h, u):
+            if u == 0:
+                g_g[b, h] = stage.tile([P, 2048], BF16, name="g_g", align_bytes=64)
+            nc.vector.tensor_copy(
+                out=g_g[b, h][:].rearrange("p (q u e t) -> p q u e t", u=2, e=2, t=PACK)[:, :, u],
+                in_=f_sb[b, h][:, :, u, :].rearrange("p t (q e) -> p q e t", e=2),
+            )
+
+        def g_quant(b, h):
+            g_q[b, h] = codes_tile("g_q%d%d" % (b, h))
+            quant(g_q[b, h], g_g[b, h], E5M2)
+
+        def t_quant(b, h):
+            t_q[b, h] = codes_tile("t_q%d%d" % (b, h))
+            quant(t_q[b, h], t_g[b, h], E5M2)
+
+        def wv_turn(i0, g, ii):
+            bank = pst.tile([P, 2, 2, P], F32, name="tr")
+            banks["w", i0, g, ii] = bank
+            for i2 in range(2):
+                words = wv_raw[i0][:, 2 * ii + i2, :].bitcast(F32)
+                for u in range(2):
+                    nc.tensor.transpose(bank[:, i2, u, :], words[:, 256 * g + u : 256 * (g + 1) : 2], id_f[:])
+
+        def wv_out(i0, g, ii, eng):
+            if ii == 0:
+                wv_g[i0, g] = stage.tile([P, 2048], BF16, name="wv_g", align_bytes=64)
+            copy(eng, wv_g[i0, g][:, 1024 * ii : 1024 * (ii + 1)].bitcast(F32).rearrange("p (i r u) -> p i r u", i=2, u=2),
+                 banks["w", i0, g, ii][:].rearrange("p i u r -> p i r u"))
+
+        def wv_quant(i0, g):
+            wv_q[i0, g] = codes_tile("wv_q%d%d" % (i0, g))
+            quant(wv_q[i0, g], wv_g[i0, g], E4M3)
+
+        def x_int(b, n, eng):
+            x_g[b, n] = stage.tile([P, 2048], BF16, name="x_g", align_bytes=64, bufs=3)
+            o = x_g[b, n][:].rearrange("p (c j) -> p c j", j=PACK)
+            i = x_raw[b][:, :, 512 * n : 512 * (n + 1)].rearrange("p j c -> p c j")
+            copy(eng, o, i)
+
+        def x_quant(b, n):
+            x_q[b, n] = codes_tile("x_q%d%d" % (b, n))
+            quant(x_q[b, n], x_g[b, n], E4M3)
+
+        ots = {}
+
+        def out0_mm(b, i, n):
+            bank = mm_bank("o0", b, i, n)
+            for h in range(H):
+                mx(bank[:], g_q[b, h][0], g_q[b, h][1], E5M2, wv_q[n, h][0], wv_q[n, h][1], E4M3,
+                   slice(P * i, P * (i + 1)), slice(0, 512), h == 0, h == H - 1)
+
+        def out0_ev(b, i, n, eng):
+            if ("o0", b, i) not in ots:
+                ot = outs.tile([P, D], F32, name="ot")
+                ots["o0", b, i] = ot
+            copy(eng, ots["o0", b, i][:, 512 * n : 512 * (n + 1)], banks["o0", b, i, n][:])
+
+        def out0_st(b, i):
+            nc.sync.dma_start(out=out_0[b, P * i : P * (i + 1), :], in_=ots["o0", b, i][:])
+
+        def out1_mm(i, h):
+            bank = mm_bank("o1", i, h)
+            for b in range(B):
+                mx(bank[:], x_q[b, i // 4][0], x_q[b, i // 4][1], E4M3, t_q[b, h][0], t_q[b, h][1], E5M2,
+                   slice(P * (i % 4), P * (i % 4 + 1)), slice(0, 512), b == 0, b == B - 1)
+
+        def out1_ev(i, h, eng):
+            if ("o1", i) not in ots:
+                ot = outs.tile([P, E], F32, name="ot")
+                ots["o1", i] = ot
+            copy(eng, ots["o1", i][:, 512 * h : 512 * (h + 1)].rearrange("p (m t) -> p m t", t=PACK),
+                 banks["o1", i, h][:].rearrange("p (t m) -> p m t", t=PACK))
+
+        def out1_st(i):
+            nc.sync.dma_start(out=out_1[P * i : P * (i + 1), :], in_=ots["o1", i][:])
+
+        load_do(0, 0)
+        load_att(0, 0)
+        gf_pe(0, 0, 2)
+        gf_pe(0, 0, 3)
+        gf_lin()
+        load_att2(0, 0)
+        load_att(0, 1)
+        do_int(0, 0, 's')
+        do_quant(0, 0)
+        gf_pe(0, 0, 0)
+        gf_sum(0, 0, 0)
+        gf_pe(0, 1, 0)
+        load_do(0, 1)
+        gf_pe(0, 0, 1)
+        gf_sum(0, 0, 1)
+        gf_pe(0, 1, 1)
+        gf_sum(0, 0, 2)
+        gf_sum(0, 0, 3)
+        gf_quant(0, 0)
+        gf_pe(0, 1, 2)
+        load_att2(0, 1)
+        feat_mm(0, 0, 0)
+        feat_mm(0, 0, 1)
+        load_wv(0)
+        gf_sum(0, 1, 0)
+        gf_sum(0, 1, 1)
+        do_int(0, 1, 's')
+        gf_pe(0, 1, 3)
+        feat_out(0, 0, 0, 's')
+        feat_out(0, 0, 1, 's')
+        feat_mm(0, 0, 2)
+        feat_out(0, 0, 2, 's')
+        feat_mm(0, 0, 3)
+        gf_sum(0, 1, 2)
+        gf_sum(0, 1, 3)
+        feat_out(0, 0, 3, 's')
+        turn(0, 0, 0)
+        turn_out(0, 0, 0, 'v')
+        load_do(1, 0)
+        gf_quant(0, 1)
+        wv_turn(0, 0, 0)
+        wv_out(0, 0, 0, 's')
+        do_quant(0, 1)
+        g_int(0, 0, 0)
+        g_int(0, 0, 1)
+        wv_turn(0, 1, 0)
+        load_att(1, 0)
+        feat_mm(0, 1, 0)
+        do_int(1, 0, 's')
+        feat_mm(0, 1, 1)
+        feat_mm(0, 1, 2)
+        feat_out(0, 1, 0, 's')
+        feat_mm(0, 1, 3)
+        feat_out(0, 1, 1, 'v')
+        feat_out(0, 1, 2, 's')
+        do_quant(1, 0)
+        wv_out(0, 1, 0, 's')
+        load_att2(1, 0)
+        load_do(1, 1)
+        gf_pe(1, 0, 0)
+        load_att(1, 1)
+        load_att2(1, 1)
+        load_x(0)
+        gf_pe(1, 0, 1)
+        g_quant(0, 0)
+        turn(0, 1, 0)
+        turn_out(0, 1, 0, 's')
+        gf_pe(1, 0, 2)
+        gf_pe(1, 0, 3)
+        gf_pe(1, 1, 1)
+        gf_sum(1, 0, 0)
+        gf_sum(1, 0, 1)
+        gf_sum(1, 0, 2)
+        gf_sum(1, 0, 3)
+        wv_turn(0, 0, 1)
+        feat_out(0, 1, 3, 's')
+        do_int(1, 1, 's')
+        wv_out(0, 0, 1, 's')
+        wv_turn(0, 1, 1)
+        wv_out(0, 1, 1, 's')
+        g_int(0, 1, 0)
+        g_int(0, 1, 1)
+        gf_quant(1, 0)
+        gf_pe(1, 1, 0)
+        gf_sum(1, 1, 0)
+        gf_pe(1, 1, 2)
+        turn(0, 1, 1)
+        gf_sum(1, 1, 1)
+        gf_sum(1, 1, 2)
+        turn(0, 0, 1)
+        do_quant(1, 1)
+        turn_out(0, 1, 1, 's')
+        turn_out(0, 0, 1, 's')
+        wv_quant(0, 0)
+        gf_pe(1, 1, 3)
+        feat_mm(1, 0, 0)
+        feat_mm(1, 0, 1)
+        gf_sum(1, 1, 3)
+        x_int(0, 1, 's')
+        feat_out(1, 0, 0, 'v')
+        feat_mm(1, 0, 2)
+        feat_mm(1, 0, 3)
+        feat_out(1, 0, 1, 's')
+        feat_out(1, 0, 2, 's')
+        load_wv(1)
+        wv_turn(1, 0, 0)
+        wv_turn(1, 0, 1)
+        load_x(1)
+        gf_quant(1, 1)
+        wv_out(1, 0, 0, 's')
+        feat_mm(1, 1, 0)
+        feat_mm(1, 1, 1)
+        feat_mm(1, 1, 2)
+        feat_out(1, 0, 3, 'v')
+        wv_turn(1, 1, 0)
+        feat_mm(1, 1, 3)
+        g_quant(0, 1)
+        wv_turn(1, 1, 1)
+        wv_quant(0, 1)
+        out0_mm(0, 1, 0)
+        g_int(1, 0, 0)
+        feat_out(1, 1, 0, 's')
+        feat_out(1, 1, 1, 'v')
+        wv_out(1, 0, 1, 's')
+        feat_out(1, 1, 2, 's')
+        wv_quant(1, 0)
+        feat_out(1, 1, 3, 's')
+        turn(1, 0, 0)
+        out0_mm(0, 0, 0)
+        wv_out(1, 1, 0, 's')
+        x_int(1, 1, 's')
+        out0_ev(0, 0, 0, 's')
+        out0_mm(0, 3, 0)
+        g_int(1, 1, 0)
+        wv_out(1, 1, 1, 'v')
+        out0_ev(0, 1, 0, 'v')
+        wv_quant(1, 1)
+        out0_mm(0, 0, 1)
+        out0_ev(0, 0, 1, 's')
+        t_quant(0, 0)
+        out0_st(0, 0)
+        out0_mm(0, 1, 1)
+        g_int(1, 1, 1)
+        out0_mm(0, 2, 0)
+        out0_ev(0, 3, 0, 's')
+        out0_mm(0, 3, 1)
+        out0_ev(0, 3, 1, 's')
+        out0_mm(0, 2, 1)
+        out0_st(0, 3)
+        g_int(1, 0, 1)
+        g_quant(1, 1)
+        turn_out(1, 0, 0, 's')
+        g_quant(1, 0)
+        turn(1, 0, 1)
+        turn_out(1, 0, 1, 'v')
+        out0_ev(0, 1, 1, 's')
+        turn(1, 1, 0)
+        turn(1, 1, 1)
+        out0_ev(0, 2, 0, 's')
+        out0_ev(0, 2, 1, 's')
+        x_quant(0, 1)
+        turn_out(1, 1, 0, 's')
+        t_quant(0, 1)
+        x_quant(1, 1)
+        turn_out(1, 1, 1, 's')
+        out0_mm(1, 0, 1)
+        out0_mm(1, 0, 0)
+        out0_mm(1, 1, 0)
+        out0_ev(1, 0, 0, 'v')
+        out0_ev(1, 0, 1, 's')
+        out0_ev(1, 1, 0, 's')
+        out0_st(0, 1)
+        out0_st(0, 2)
+        t_quant(1, 0)
+        out0_mm(1, 1, 1)
+        t_quant(1, 1)
+        out1_mm(6, 0)
+        out1_mm(6, 1)
+        out1_ev(6, 0, 'v')
+        out1_ev(6, 1, 'v')
+        out1_mm(5, 0)
+        out1_ev(5, 0, 'v')
+        out0_st(1, 0)
+        out0_ev(1, 1, 1, 's')
+        out0_st(1, 1)
+        out1_mm(5, 1)
+        out1_ev(5, 1, 'v')
+        out1_st(6)
+        out0_mm(1, 2, 0)
+        out0_ev(1, 2, 0, 'v')
+        x_int(1, 0, 's')
+        out0_mm(1, 2, 1)
+        out0_mm(1, 3, 1)
+        out0_ev(1, 2, 1, 's')
+        out0_mm(1, 3, 0)
+        out0_ev(1, 3, 0, 's')
+        out0_ev(1, 3, 1, 's')
+        out1_mm(7, 0)
+        out1_mm(4, 0)
+        out1_st(5)
+        out0_st(1, 2)
+        out1_mm(7, 1)
+        x_int(0, 0, 'v')
+        x_quant(1, 0)
+        x_quant(0, 0)
+        out0_st(1, 3)
+        out1_mm(4, 1)
+        out1_ev(7, 0, 'v')
+        out1_ev(7, 1, 's')
+        out1_st(7)
+        out1_ev(4, 0, 'v')
+        out1_mm(3, 0)
+        out1_ev(3, 0, 's')
+        out1_mm(1, 0)
+        out1_mm(1, 1)
+        out1_ev(1, 0, 's')
+        out1_mm(3, 1)
+        out1_ev(4, 1, 'v')
+        out1_ev(3, 1, 's')
+        out1_st(4)
+        out1_ev(1, 1, 'v')
+        out1_st(1)
+        out1_st(3)
+        out1_mm(0, 0)
+        out1_mm(2, 0)
+        out1_ev(2, 0, 'v')
+        out1_mm(2, 1)
+        out1_mm(0, 1)
+        out1_ev(2, 1, 'v')
+        out1_ev(0, 0, 's')
+        out1_ev(0, 1, 's')
+        out1_st(2)
+        out1_st(0)

@@ -31,10 +31,12 @@ def tile_gfsa_pa_v_kernel(tc, x, att, Wv, bv, w0, w1, wK, att2, grad_out, out_0,
         ctx.enter_context(tc.manual_schedule())
 
         wt = {}
-        for nm, src in (("w0", w0), ("w1", w1), ("wK", wK)):
-            t = const.tile([P, H], BF16, name="wt_" + nm)
-            nc.scalar.dma_start(out=t[:], in_=src.partition_broadcast(P))
-            wt[nm] = t
+
+        def load_w():
+            for nm, src in (("w0", w0), ("w1", w1), ("wK", wK)):
+                t = const.tile([P, H], BF16, name="wt_" + nm)
+                nc.sync.dma_start(out=t[:], in_=src.partition_broadcast(P))
+                wt[nm] = t
 
         do_raw = {}
         att_sb = {}
@@ -44,7 +46,13 @@ def tile_gfsa_pa_v_kernel(tc, x, att, Wv, bv, w0, w1, wK, att2, grad_out, out_0,
         def load_do(b, h):
             t = raw.tile([P, PACK, DH], BF16, name="do_raw%d%d" % (b, h))
             nc.sync.dma_start(out=t[:], in_=grad_out[b, :, DH * h : DH * (h + 1)].rearrange("(p j) e -> p j e", j=PACK))
-            do_raw[b, h] = t
+            do_raw[b, h] = t[:]
+
+        def load_do_both(b):
+            t = raw.tile([P, PACK, E], BF16, name="do_raw%d" % b)
+            nc.sync.dma_start(out=t[:], in_=grad_out[b].rearrange("(p j) e -> p j e", j=PACK))
+            for h in range(H):
+                do_raw[b, h] = t[:, :, DH * h : DH * (h + 1)]
 
         def load_att(b, h):
             t = raw.tile([P, PACK, N], BF16, name="att_sb", bufs=3)
@@ -76,28 +84,30 @@ def tile_gfsa_pa_v_kernel(tc, x, att, Wv, bv, w0, w1, wK, att2, grad_out, out_0,
         for j in range(PACK):
             nc.vector.tensor_copy(out=irep[:, j, :], in_=id_bf[:])
         diag = {}
-        for h in range(H):
-            for nm, sgn in (("w1", 1.0), ("wK", -1.0), ("w0", 1.0)):
-                t = const.tile([P, P], BF16, name="diag_%s%d" % (nm, h))
-                nc.vector.tensor_scalar(out=t[:], in0=id_bf[:], scalar1=wt[nm][:, h : h + 1], scalar2=sgn, op0=ALU.mult, op1=ALU.mult)
-                diag[nm, h] = t
         wk2 = const.tile([P, H], F32)
-        nc.vector.tensor_scalar(out=wk2[:], in0=wt["wK"][:], scalar1=2.0, scalar2=None, op0=ALU.mult)
         c1 = const.tile([P, H], F32)
-        nc.vector.tensor_tensor(out=c1[:], in0=wt["w1"][:], in1=wt["wK"][:], op=ALU.subtract)
         w0f = const.tile([P, H], F32)
-        nc.vector.tensor_copy(out=w0f[:], in_=wt["w0"][:])
         KD = 256
         dmask = const.tile([P, PACK * (KD + 1)], F32)
         nc.gpsimd.memset(dmask[:], 0.0)
-        nc.gpsimd.tensor_scalar(
-            out=dmask[:].rearrange("p (j x) -> p j x", x=KD + 1)[:, :, 0:KD:PACK],
-            in0=irep[:, :, 0 : KD // PACK],
-            scalar1=w0f[:, 0:1],
-            scalar2=0.0,
-            op0=ALU.mult,
-            op1=ALU.add,
-        )
+
+        def consts(h):
+            for nm, sgn in (("w1", 1.0), ("wK", -1.0), ("w0", 1.0)):
+                t = const.tile([P, P], BF16, name="diag_%s%d" % (nm, h))
+                nc.gpsimd.tensor_scalar(out=t[:], in0=id_bf[:], scalar1=wt[nm][:, h : h + 1], scalar2=sgn, op0=ALU.mult, op1=ALU.mult)
+                diag[nm, h] = t
+            if h == 0:
+                nc.gpsimd.tensor_scalar(out=wk2[:], in0=wt["wK"][:], scalar1=2.0, scalar2=0.0, op0=ALU.mult, op1=ALU.add)
+                nc.gpsimd.tensor_tensor(out=c1[:], in0=wt["w1"][:], in1=wt["wK"][:], op=ALU.subtract)
+                nc.gpsimd.tensor_copy(out=w0f[:], in_=wt["w0"][:])
+                nc.gpsimd.tensor_scalar(
+                    out=dmask[:].rearrange("p (j x) -> p j x", x=KD + 1)[:, :, 0:KD:PACK],
+                    in0=irep[:, :, 0 : KD // PACK],
+                    scalar1=w0f[:, 0:1],
+                    scalar2=0.0,
+                    op0=ALU.mult,
+                    op1=ALU.add,
+                )
 
         def codes_tile(name, bufs=1):
             c = keep.tile([P, 512], U32, name=name + "_c", align_bytes=64, bufs=bufs)
@@ -119,8 +129,8 @@ def tile_gfsa_pa_v_kernel(tc, x, att, Wv, bv, w0, w1, wK, att2, grad_out, out_0,
 
         def do_int(b, h, eng):
             t = stage.tile([P, 2048], BF16, name="do_g", align_bytes=64)
-            copy(eng, t[:].rearrange("p (t m j) -> p t m j", t=PACK, j=PACK),
-                 do_raw[b, h][:].rearrange("p j (m t) -> p t m j", t=PACK))
+            copy(eng, t[:].rearrange("p (t m j) -> p m t j", t=PACK, j=PACK),
+                 do_raw[b, h].rearrange("p j (m t) -> p m t j", t=PACK))
             do_g[b, h] = t
 
         def do_quant(b, h):
@@ -194,17 +204,16 @@ def tile_gfsa_pa_v_kernel(tc, x, att, Wv, bv, w0, w1, wK, att2, grad_out, out_0,
 
         def feat_out(b, h, t, eng):
             if t == 0:
-                f_sb[b, h] = stage.tile([P, PACK, 2, 256], BF16, name="f_sb", align_bytes=64)
-            copy(eng, f_sb[b, h][:, t].rearrange("p u (q e) -> p u q e", e=2),
-                 banks["f", b, h, t][:].rearrange("p (q u e) -> p u q e", u=2, e=2))
+                f_sb[b, h] = stage.tile([P, PACK, N], BF16, name="f_sb", align_bytes=64)
+            copy(eng, f_sb[b, h][:, t, :], banks["f", b, h, t][:])
 
         def turn(b, h, tt):
             bank = pst.tile([P, 2, 2, P], F32, name="tr")
             banks["t", b, h, tt] = bank
             for t2 in range(2):
-                words = f_sb[b, h][:, 2 * tt + t2].rearrange("p u w -> p (u w)").bitcast(F32)
+                words = f_sb[b, h][:, 2 * tt + t2, :].bitcast(F32)
                 for u in range(2):
-                    nc.tensor.transpose(bank[:, t2, u, :], words[:, P * u : P * (u + 1)], id_f[:])
+                    nc.tensor.transpose(bank[:, t2, u, :], words[:, u::2], id_f[:])
 
         def turn_out(b, h, tt, eng):
             if tt == 0:
@@ -212,12 +221,11 @@ def tile_gfsa_pa_v_kernel(tc, x, att, Wv, bv, w0, w1, wK, att2, grad_out, out_0,
             copy(eng, t_g[b, h][:, 1024 * tt : 1024 * (tt + 1)].bitcast(F32).rearrange("p (t r u) -> p t r u", t=2, u=2),
                  banks["t", b, h, tt][:].rearrange("p t u r -> p t r u"))
 
-        def g_int(b, h, u):
-            if u == 0:
-                g_g[b, h] = stage.tile([P, 2048], BF16, name="g_g", align_bytes=64)
+        def g_int(b, h):
+            g_g[b, h] = stage.tile([P, 2048], BF16, name="g_g", align_bytes=64)
             nc.vector.tensor_copy(
-                out=g_g[b, h][:].rearrange("p (q u e t) -> p q u e t", u=2, e=2, t=PACK)[:, :, u],
-                in_=f_sb[b, h][:, :, u, :].rearrange("p t (q e) -> p q e t", e=2),
+                out=g_g[b, h][:].rearrange("p (c i t) -> p c t i", i=4, t=PACK),
+                in_=f_sb[b, h][:].rearrange("p t (c i) -> p c t i", i=4),
             )
 
         def g_quant(b, h):
@@ -248,9 +256,8 @@ def tile_gfsa_pa_v_kernel(tc, x, att, Wv, bv, w0, w1, wK, att2, grad_out, out_0,
 
         def x_int(b, n, eng):
             x_g[b, n] = stage.tile([P, 2048], BF16, name="x_g", align_bytes=64, bufs=3)
-            o = x_g[b, n][:].rearrange("p (c j) -> p c j", j=PACK)
-            i = x_raw[b][:, :, 512 * n : 512 * (n + 1)].rearrange("p j c -> p c j")
-            copy(eng, o, i)
+            copy(eng, x_g[b, n][:].rearrange("p (c i j) -> p c j i", i=4, j=PACK),
+                 x_raw[b][:, :, 512 * n : 512 * (n + 1)].rearrange("p j (c i) -> p c j i", i=4))
 
         def x_quant(b, n):
             x_q[b, n] = codes_tile("x_q%d%d" % (b, n))
@@ -290,235 +297,233 @@ def tile_gfsa_pa_v_kernel(tc, x, att, Wv, bv, w0, w1, wK, att2, grad_out, out_0,
             nc.sync.dma_start(out=out_1[P * i : P * (i + 1), :], in_=ots["o1", i][:])
 
         load_do(0, 0)
-        load_att(0, 0)
-        gf_pe(0, 0, 2)
-        gf_pe(0, 0, 3)
-        gf_lin()
-        load_att2(0, 0)
-        load_att(0, 1)
         do_int(0, 0, 's')
         do_quant(0, 0)
-        gf_pe(0, 0, 0)
-        gf_sum(0, 0, 0)
-        gf_pe(0, 1, 0)
         load_do(0, 1)
-        gf_pe(0, 0, 1)
-        gf_sum(0, 0, 1)
+        do_int(0, 1, 'v')
+        load_w()
+        consts(1)
+        load_att(0, 1)
+        gf_pe(0, 1, 3)
+        gf_pe(0, 1, 0)
         gf_pe(0, 1, 1)
-        gf_sum(0, 0, 2)
-        gf_sum(0, 0, 3)
-        gf_quant(0, 0)
         gf_pe(0, 1, 2)
         load_att2(0, 1)
-        feat_mm(0, 0, 0)
-        feat_mm(0, 0, 1)
-        load_wv(0)
+        consts(0)
         gf_sum(0, 1, 0)
-        gf_sum(0, 1, 1)
-        do_int(0, 1, 's')
-        gf_pe(0, 1, 3)
-        feat_out(0, 0, 0, 's')
-        feat_out(0, 0, 1, 's')
-        feat_mm(0, 0, 2)
-        feat_out(0, 0, 2, 's')
-        feat_mm(0, 0, 3)
-        gf_sum(0, 1, 2)
-        gf_sum(0, 1, 3)
-        feat_out(0, 0, 3, 's')
-        turn(0, 0, 0)
-        turn_out(0, 0, 0, 'v')
-        load_do(1, 0)
-        gf_quant(0, 1)
+        load_wv(0)
         wv_turn(0, 0, 0)
         wv_out(0, 0, 0, 's')
-        do_quant(0, 1)
-        g_int(0, 0, 0)
-        g_int(0, 0, 1)
+        gf_sum(0, 1, 1)
+        gf_sum(0, 1, 2)
+        gf_sum(0, 1, 3)
         wv_turn(0, 1, 0)
-        load_att(1, 0)
-        feat_mm(0, 1, 0)
-        do_int(1, 0, 's')
-        feat_mm(0, 1, 1)
-        feat_mm(0, 1, 2)
-        feat_out(0, 1, 0, 's')
-        feat_mm(0, 1, 3)
-        feat_out(0, 1, 1, 'v')
-        feat_out(0, 1, 2, 's')
-        do_quant(1, 0)
-        wv_out(0, 1, 0, 's')
-        load_att2(1, 0)
-        load_do(1, 1)
-        gf_pe(1, 0, 0)
-        load_att(1, 1)
-        load_att2(1, 1)
-        load_x(0)
-        gf_pe(1, 0, 1)
-        g_quant(0, 0)
-        turn(0, 1, 0)
-        turn_out(0, 1, 0, 's')
-        gf_pe(1, 0, 2)
-        gf_pe(1, 0, 3)
-        gf_pe(1, 1, 1)
-        gf_sum(1, 0, 0)
-        gf_sum(1, 0, 1)
-        gf_sum(1, 0, 2)
-        gf_sum(1, 0, 3)
+        load_att(0, 0)
+        gf_pe(0, 0, 3)
         wv_turn(0, 0, 1)
-        feat_out(0, 1, 3, 's')
-        do_int(1, 1, 's')
-        wv_out(0, 0, 1, 's')
+        do_quant(0, 1)
+        gf_quant(0, 1)
+        feat_mm(0, 1, 0)
+        feat_mm(0, 1, 1)
         wv_turn(0, 1, 1)
-        wv_out(0, 1, 1, 's')
-        g_int(0, 1, 0)
-        g_int(0, 1, 1)
-        gf_quant(1, 0)
-        gf_pe(1, 1, 0)
-        gf_sum(1, 1, 0)
-        gf_pe(1, 1, 2)
-        turn(0, 1, 1)
-        gf_sum(1, 1, 1)
-        gf_sum(1, 1, 2)
-        turn(0, 0, 1)
-        do_quant(1, 1)
-        turn_out(0, 1, 1, 's')
-        turn_out(0, 0, 1, 's')
-        wv_quant(0, 0)
-        gf_pe(1, 1, 3)
-        feat_mm(1, 0, 0)
-        feat_mm(1, 0, 1)
-        gf_sum(1, 1, 3)
-        x_int(0, 1, 's')
-        feat_out(1, 0, 0, 'v')
-        feat_mm(1, 0, 2)
-        feat_mm(1, 0, 3)
-        feat_out(1, 0, 1, 's')
-        feat_out(1, 0, 2, 's')
+        load_att2(0, 0)
+        gf_pe(0, 0, 2)
+        wv_out(0, 1, 0, 's')
         load_wv(1)
+        gf_lin()
+        gf_pe(0, 0, 0)
+        gf_sum(0, 0, 0)
+        load_att(1, 0)
+        wv_out(0, 0, 1, 's')
+        load_do_both(1)
+        feat_mm(0, 1, 2)
+        feat_mm(0, 1, 3)
+        gf_pe(0, 0, 1)
+        gf_sum(0, 0, 1)
+        load_att2(1, 0)
         wv_turn(1, 0, 0)
         wv_turn(1, 0, 1)
+        feat_out(0, 1, 0, 's')
+        wv_out(0, 1, 1, 's')
+        load_att(1, 1)
+        gf_sum(0, 0, 2)
+        feat_out(0, 1, 1, 's')
+        feat_out(0, 1, 2, 's')
+        feat_out(0, 1, 3, 's')
+        gf_sum(0, 0, 3)
+        gf_quant(0, 0)
+        feat_mm(0, 0, 0)
+        feat_mm(0, 0, 1)
+        feat_out(0, 0, 0, 's')
+        feat_mm(0, 0, 2)
+        feat_mm(0, 0, 3)
         load_x(1)
-        gf_quant(1, 1)
-        wv_out(1, 0, 0, 's')
-        feat_mm(1, 1, 0)
-        feat_mm(1, 1, 1)
-        feat_mm(1, 1, 2)
-        feat_out(1, 0, 3, 'v')
         wv_turn(1, 1, 0)
-        feat_mm(1, 1, 3)
-        g_quant(0, 1)
-        wv_turn(1, 1, 1)
+        load_att2(1, 1)
+        gf_pe(1, 0, 0)
+        wv_quant(0, 0)
         wv_quant(0, 1)
-        out0_mm(0, 1, 0)
-        g_int(1, 0, 0)
-        feat_out(1, 1, 0, 's')
-        feat_out(1, 1, 1, 'v')
+        wv_out(1, 0, 0, 's')
+        gf_pe(1, 0, 1)
         wv_out(1, 0, 1, 's')
-        feat_out(1, 1, 2, 's')
+        feat_out(0, 0, 1, 'v')
+        turn(0, 0, 0)
+        feat_out(0, 0, 2, 'v')
+        gf_pe(1, 0, 3)
         wv_quant(1, 0)
-        feat_out(1, 1, 3, 's')
-        turn(1, 0, 0)
-        out0_mm(0, 0, 0)
+        feat_out(0, 0, 3, 's')
         wv_out(1, 1, 0, 's')
+        do_int(1, 0, 's')
+        wv_turn(1, 1, 1)
+        g_int(0, 0)
+        g_int(0, 1)
+        gf_pe(1, 1, 0)
+        gf_pe(1, 1, 1)
+        load_x(0)
+        gf_sum(1, 0, 0)
+        wv_out(1, 1, 1, 's')
+        g_quant(0, 0)
+        do_int(1, 1, 's')
+        gf_sum(1, 0, 1)
+        g_quant(0, 1)
+        do_quant(1, 0)
         x_int(1, 1, 's')
+        gf_pe(1, 0, 2)
+        gf_sum(1, 0, 2)
+        gf_sum(1, 0, 3)
+        gf_sum(1, 1, 0)
+        turn_out(0, 0, 0, 's')
+        gf_pe(1, 1, 3)
+        out0_mm(0, 0, 0)
         out0_ev(0, 0, 0, 's')
-        out0_mm(0, 3, 0)
-        g_int(1, 1, 0)
-        wv_out(1, 1, 1, 'v')
-        out0_ev(0, 1, 0, 'v')
+        out0_mm(0, 1, 0)
+        gf_pe(1, 1, 2)
+        gf_sum(1, 1, 1)
         wv_quant(1, 1)
         out0_mm(0, 0, 1)
+        turn(0, 1, 0)
+        turn(0, 1, 1)
+        gf_quant(1, 0)
+        feat_mm(1, 0, 0)
+        feat_mm(1, 0, 1)
+        gf_sum(1, 1, 2)
+        gf_sum(1, 1, 3)
+        out0_ev(0, 1, 0, 's')
+        do_quant(1, 1)
+        x_int(0, 0, 's')
+        turn_out(0, 1, 0, 'v')
         out0_ev(0, 0, 1, 's')
-        t_quant(0, 0)
+        gf_quant(1, 1)
         out0_st(0, 0)
+        feat_out(1, 0, 0, 's')
+        feat_mm(1, 0, 2)
+        feat_out(1, 0, 1, 'v')
         out0_mm(0, 1, 1)
-        g_int(1, 1, 1)
-        out0_mm(0, 2, 0)
-        out0_ev(0, 3, 0, 's')
-        out0_mm(0, 3, 1)
-        out0_ev(0, 3, 1, 's')
-        out0_mm(0, 2, 1)
-        out0_st(0, 3)
-        g_int(1, 0, 1)
-        g_quant(1, 1)
-        turn_out(1, 0, 0, 's')
-        g_quant(1, 0)
-        turn(1, 0, 1)
-        turn_out(1, 0, 1, 'v')
-        out0_ev(0, 1, 1, 's')
-        turn(1, 1, 0)
-        turn(1, 1, 1)
-        out0_ev(0, 2, 0, 's')
-        out0_ev(0, 2, 1, 's')
-        x_quant(0, 1)
-        turn_out(1, 1, 0, 's')
+        out0_ev(0, 1, 1, 'v')
+        feat_mm(1, 0, 3)
+        x_quant(0, 0)
+        feat_out(1, 0, 2, 'v')
+        feat_out(1, 0, 3, 'v')
+        turn(0, 0, 1)
+        turn_out(0, 1, 1, 's')
         t_quant(0, 1)
+        feat_mm(1, 1, 0)
+        feat_mm(1, 1, 1)
+        out0_mm(0, 3, 0)
+        out0_ev(0, 3, 0, 'v')
+        feat_out(1, 1, 0, 's')
+        turn_out(0, 0, 1, 's')
+        turn(1, 0, 0)
+        x_int(1, 0, 's')
+        feat_out(1, 1, 1, 's')
+        out0_mm(0, 2, 0)
+        feat_mm(1, 1, 2)
+        turn_out(1, 0, 0, 's')
+        turn(1, 0, 1)
+        t_quant(0, 0)
+        turn_out(1, 0, 1, 'v')
+        feat_mm(1, 1, 3)
+        out0_mm(0, 3, 1)
+        feat_out(1, 1, 2, 's')
+        x_quant(1, 0)
+        feat_out(1, 1, 3, 'v')
+        t_quant(1, 0)
+        out0_mm(0, 2, 1)
+        turn(1, 1, 0)
+        turn_out(1, 1, 0, 'v')
+        out0_ev(0, 3, 1, 's')
+        out0_ev(0, 2, 0, 's')
+        turn(1, 1, 1)
+        out0_st(0, 1)
+        out0_st(0, 3)
         x_quant(1, 1)
         turn_out(1, 1, 1, 's')
-        out0_mm(1, 0, 1)
-        out0_mm(1, 0, 0)
-        out0_mm(1, 1, 0)
-        out0_ev(1, 0, 0, 'v')
-        out0_ev(1, 0, 1, 's')
-        out0_ev(1, 1, 0, 's')
-        out0_st(0, 1)
+        out0_ev(0, 2, 1, 's')
         out0_st(0, 2)
-        t_quant(1, 0)
-        out0_mm(1, 1, 1)
-        t_quant(1, 1)
-        out1_mm(6, 0)
-        out1_mm(6, 1)
-        out1_ev(6, 0, 'v')
-        out1_ev(6, 1, 'v')
-        out1_mm(5, 0)
-        out1_ev(5, 0, 'v')
-        out0_st(1, 0)
-        out0_ev(1, 1, 1, 's')
-        out0_st(1, 1)
-        out1_mm(5, 1)
-        out1_ev(5, 1, 'v')
-        out1_st(6)
-        out0_mm(1, 2, 0)
-        out0_ev(1, 2, 0, 'v')
-        x_int(1, 0, 's')
-        out0_mm(1, 2, 1)
-        out0_mm(1, 3, 1)
-        out0_ev(1, 2, 1, 's')
-        out0_mm(1, 3, 0)
-        out0_ev(1, 3, 0, 's')
-        out0_ev(1, 3, 1, 's')
-        out1_mm(7, 0)
-        out1_mm(4, 0)
-        out1_st(5)
-        out0_st(1, 2)
-        out1_mm(7, 1)
-        x_int(0, 0, 'v')
-        x_quant(1, 0)
-        x_quant(0, 0)
-        out0_st(1, 3)
-        out1_mm(4, 1)
-        out1_ev(7, 0, 'v')
-        out1_ev(7, 1, 's')
-        out1_st(7)
-        out1_ev(4, 0, 'v')
         out1_mm(3, 0)
-        out1_ev(3, 0, 's')
-        out1_mm(1, 0)
-        out1_mm(1, 1)
-        out1_ev(1, 0, 's')
-        out1_mm(3, 1)
-        out1_ev(4, 1, 'v')
-        out1_ev(3, 1, 's')
-        out1_st(4)
-        out1_ev(1, 1, 'v')
-        out1_st(1)
-        out1_st(3)
-        out1_mm(0, 0)
         out1_mm(2, 0)
-        out1_ev(2, 0, 'v')
+        t_quant(1, 1)
+        x_int(0, 1, 'v')
+        x_quant(0, 1)
         out1_mm(2, 1)
+        out1_ev(2, 0, 's')
+        out1_ev(2, 1, 's')
+        out1_st(2)
+        g_int(1, 0)
+        g_int(1, 1)
+        out1_mm(3, 1)
         out1_mm(0, 1)
-        out1_ev(2, 1, 'v')
+        out1_ev(3, 0, 's')
+        out1_ev(3, 1, 's')
+        out1_mm(0, 0)
         out1_ev(0, 0, 's')
         out1_ev(0, 1, 's')
-        out1_st(2)
+        out1_mm(7, 0)
+        out1_ev(7, 0, 's')
+        out1_mm(7, 1)
+        g_quant(1, 0)
+        out1_st(3)
+        out1_ev(7, 1, 's')
+        out1_mm(4, 0)
+        out1_ev(4, 0, 's')
+        out1_mm(4, 1)
+        out1_mm(6, 0)
+        out1_ev(4, 1, 's')
+        out1_ev(6, 0, 's')
         out1_st(0)
+        out1_st(7)
+        out1_mm(6, 1)
+        out1_ev(6, 1, 's')
+        g_quant(1, 1)
+        out0_mm(1, 0, 0)
+        out0_mm(1, 3, 1)
+        out1_st(4)
+        out0_ev(1, 0, 0, 's')
+        out0_mm(1, 0, 1)
+        out0_ev(1, 0, 1, 'v')
+        out0_mm(1, 1, 1)
+        out1_st(6)
+        out0_st(1, 0)
+        out0_mm(1, 3, 0)
+        out0_ev(1, 3, 0, 'v')
+        out0_ev(1, 3, 1, 's')
+        out0_st(1, 3)
+        out1_mm(1, 0)
+        out1_ev(1, 0, 's')
+        out1_mm(1, 1)
+        out1_ev(1, 1, 's')
+        out0_mm(1, 1, 0)
+        out0_ev(1, 1, 0, 's')
+        out0_ev(1, 1, 1, 'v')
+        out0_mm(1, 2, 0)
+        out0_ev(1, 2, 0, 's')
+        out0_mm(1, 2, 1)
+        out1_mm(5, 1)
+        out1_st(1)
+        out0_st(1, 1)
+        out0_ev(1, 2, 1, 'v')
+        out0_st(1, 2)
+        out1_mm(5, 0)
+        out1_ev(5, 0, 's')
+        out1_ev(5, 1, 's')
+        out1_st(5)

@@ -71,10 +71,11 @@ def tile_gfsa_pa_v_kernel(tc, x, att, Wv, bv, w0, w1, wK, att2, grad_out, out_0,
 
         wv_raw = {}
 
-        def load_wv(i0):
-            t = raw.tile([P, 4, E], BF16, name="wv_raw%d" % i0)
-            nc.sync.dma_start(out=t[:], in_=Wv[512 * i0 : 512 * (i0 + 1), :].rearrange("(i p) e -> p i e", p=P))
-            wv_raw[i0] = t
+        def load_wv(i0, ii):
+            t = raw.tile([P, 2, E], BF16, name="wv_raw%d%d" % (i0, ii))
+            r = 512 * i0 + 256 * ii
+            nc.sync.dma_start(out=t[:], in_=Wv[r : r + 256, :].rearrange("(i p) e -> p i e", p=P))
+            wv_raw[i0, ii] = t
 
         id_bf = const.tile([P, P], BF16)
         make_identity(nc, id_bf[:])
@@ -218,8 +219,8 @@ def tile_gfsa_pa_v_kernel(tc, x, att, Wv, bv, w0, w1, wK, att2, grad_out, out_0,
         def turn_out(b, h, tt, eng):
             if tt == 0:
                 t_g[b, h] = stage.tile([P, 2048], BF16, name="t_g", align_bytes=64)
-            copy(eng, t_g[b, h][:, 1024 * tt : 1024 * (tt + 1)].bitcast(F32).rearrange("p (t r u) -> p t r u", t=2, u=2),
-                 banks["t", b, h, tt][:].rearrange("p t u r -> p t r u"))
+            copy(eng, t_g[b, h][:, 1024 * tt : 1024 * (tt + 1)].bitcast(F32).rearrange("p (r t u) -> p r t u", t=2, u=2),
+                 banks["t", b, h, tt][:].rearrange("p t u r -> p r t u"))
 
         def g_int(b, h):
             g_g[b, h] = stage.tile([P, 2048], BF16, name="g_g", align_bytes=64)
@@ -240,7 +241,7 @@ def tile_gfsa_pa_v_kernel(tc, x, att, Wv, bv, w0, w1, wK, att2, grad_out, out_0,
             bank = pst.tile([P, 2, 2, P], F32, name="tr")
             banks["w", i0, g, ii] = bank
             for i2 in range(2):
-                words = wv_raw[i0][:, 2 * ii + i2, :].bitcast(F32)
+                words = wv_raw[i0, ii][:, i2, :].bitcast(F32)
                 for u in range(2):
                     nc.tensor.transpose(bank[:, i2, u, :], words[:, 256 * g + u : 256 * (g + 1) : 2], id_f[:])
 
@@ -265,11 +266,10 @@ def tile_gfsa_pa_v_kernel(tc, x, att, Wv, bv, w0, w1, wK, att2, grad_out, out_0,
 
         ots = {}
 
-        def out0_mm(b, i, n):
-            bank = mm_bank("o0", b, i, n)
-            for h in range(H):
-                mx(bank[:], g_q[b, h][0], g_q[b, h][1], E5M2, wv_q[n, h][0], wv_q[n, h][1], E4M3,
-                   slice(P * i, P * (i + 1)), slice(0, 512), h == 0, h == H - 1)
+        def out0_mm(b, i, n, h):
+            bank = mm_bank("o0", b, i, n) if h == 0 else banks["o0", b, i, n]
+            mx(bank[:], g_q[b, h][0], g_q[b, h][1], E5M2, wv_q[n, h][0], wv_q[n, h][1], E4M3,
+               slice(P * i, P * (i + 1)), slice(0, 512), h == 0, h == H - 1)
 
         def out0_ev(b, i, n, eng):
             if ("o0", b, i) not in ots:
@@ -280,250 +280,287 @@ def tile_gfsa_pa_v_kernel(tc, x, att, Wv, bv, w0, w1, wK, att2, grad_out, out_0,
         def out0_st(b, i):
             nc.sync.dma_start(out=out_0[b, P * i : P * (i + 1), :], in_=ots["o0", b, i][:])
 
-        def out1_mm(i, h):
-            bank = mm_bank("o1", i, h)
-            for b in range(B):
-                mx(bank[:], x_q[b, i // 4][0], x_q[b, i // 4][1], E4M3, t_q[b, h][0], t_q[b, h][1], E5M2,
-                   slice(P * (i % 4), P * (i % 4 + 1)), slice(0, 512), b == 0, b == B - 1)
+        def out1_mm(i, h, b):
+            bank = mm_bank("o1", i, h) if b == 0 else banks["o1", i, h]
+            mx(bank[:], x_q[b, i // 4][0], x_q[b, i // 4][1], E4M3, t_q[b, h][0], t_q[b, h][1], E5M2,
+               slice(P * (i % 4), P * (i % 4 + 1)), slice(0, 512), b == 0, b == B - 1)
 
         def out1_ev(i, h, eng):
             if ("o1", i) not in ots:
                 ot = outs.tile([P, E], F32, name="ot")
                 ots["o1", i] = ot
-            copy(eng, ots["o1", i][:, 512 * h : 512 * (h + 1)].rearrange("p (m t) -> p m t", t=PACK),
-                 banks["o1", i, h][:].rearrange("p (t m) -> p m t", t=PACK))
+            copy(eng, ots["o1", i][:, 512 * h : 512 * (h + 1)].rearrange("p (m t v) -> p m t v", t=2, v=2),
+                 banks["o1", i, h][:].rearrange("p (t m v) -> p m t v", t=2, v=2))
 
         def out1_st(i):
             nc.sync.dma_start(out=out_1[P * i : P * (i + 1), :], in_=ots["o1", i][:])
 
+        def out1_half(i, h):
+            nc.sync.dma_start(out=out_1[P * i : P * (i + 1), 512 * h : 512 * (h + 1)], in_=ots["o1", i][:, 512 * h : 512 * (h + 1)])
+
         load_do(0, 0)
-        do_int(0, 0, 's')
+        do_int(0, 0, 'v')
         do_quant(0, 0)
-        load_do(0, 1)
-        do_int(0, 1, 'v')
         load_w()
+        load_att(0, 0)
+        consts(0)
         consts(1)
+        gf_pe(0, 0, 2)
+        load_att2(0, 0)
+        gf_lin()
         load_att(0, 1)
-        gf_pe(0, 1, 3)
+        gf_pe(0, 0, 3)
         gf_pe(0, 1, 0)
+        load_do(0, 1)
+        do_int(0, 1, 's')
+        gf_pe(0, 0, 0)
+        gf_pe(0, 0, 1)
+        gf_sum(0, 0, 0)
+        gf_sum(0, 0, 1)
         gf_pe(0, 1, 1)
         gf_pe(0, 1, 2)
-        load_att2(0, 1)
-        consts(0)
-        gf_sum(0, 1, 0)
-        load_wv(0)
-        wv_turn(0, 0, 0)
-        wv_out(0, 0, 0, 's')
-        gf_sum(0, 1, 1)
-        gf_sum(0, 1, 2)
-        gf_sum(0, 1, 3)
-        wv_turn(0, 1, 0)
-        load_att(0, 0)
-        gf_pe(0, 0, 3)
-        wv_turn(0, 0, 1)
-        do_quant(0, 1)
-        gf_quant(0, 1)
-        feat_mm(0, 1, 0)
-        feat_mm(0, 1, 1)
-        wv_turn(0, 1, 1)
-        load_att2(0, 0)
-        gf_pe(0, 0, 2)
-        wv_out(0, 1, 0, 's')
-        load_wv(1)
-        gf_lin()
-        gf_pe(0, 0, 0)
-        gf_sum(0, 0, 0)
-        load_att(1, 0)
-        wv_out(0, 0, 1, 's')
-        load_do_both(1)
-        feat_mm(0, 1, 2)
-        feat_mm(0, 1, 3)
-        gf_pe(0, 0, 1)
-        gf_sum(0, 0, 1)
-        load_att2(1, 0)
-        wv_turn(1, 0, 0)
-        wv_turn(1, 0, 1)
-        feat_out(0, 1, 0, 's')
-        wv_out(0, 1, 1, 's')
-        load_att(1, 1)
         gf_sum(0, 0, 2)
-        feat_out(0, 1, 1, 's')
-        feat_out(0, 1, 2, 's')
-        feat_out(0, 1, 3, 's')
         gf_sum(0, 0, 3)
         gf_quant(0, 0)
         feat_mm(0, 0, 0)
         feat_mm(0, 0, 1)
-        feat_out(0, 0, 0, 's')
+        load_wv(0, 0)
+        wv_turn(0, 0, 0)
+        wv_out(0, 0, 0, 's')
         feat_mm(0, 0, 2)
-        feat_mm(0, 0, 3)
-        load_x(1)
-        wv_turn(1, 1, 0)
-        load_att2(1, 1)
-        gf_pe(1, 0, 0)
-        wv_quant(0, 0)
-        wv_quant(0, 1)
-        wv_out(1, 0, 0, 's')
-        gf_pe(1, 0, 1)
-        wv_out(1, 0, 1, 's')
-        feat_out(0, 0, 1, 'v')
+        wv_turn(0, 1, 0)
+        feat_out(0, 0, 0, 'v')
+        load_att2(0, 1)
+        do_quant(0, 1)
+        feat_out(0, 0, 1, 's')
         turn(0, 0, 0)
-        feat_out(0, 0, 2, 'v')
-        gf_pe(1, 0, 3)
-        wv_quant(1, 0)
+        load_wv(1, 0)
+        gf_pe(0, 1, 3)
+        wv_out(0, 1, 0, 's')
+        gf_sum(0, 1, 0)
+        feat_out(0, 0, 2, 's')
+        load_wv(0, 1)
+        feat_mm(0, 0, 3)
+        wv_turn(0, 1, 1)
+        turn_out(0, 0, 0, 's')
+        wv_turn(0, 0, 1)
+        gf_sum(0, 1, 1)
+        gf_sum(0, 1, 2)
+        gf_sum(0, 1, 3)
+        gf_quant(0, 1)
+        load_do_both(1)
         feat_out(0, 0, 3, 's')
-        wv_out(1, 1, 0, 's')
-        do_int(1, 0, 's')
-        wv_turn(1, 1, 1)
         g_int(0, 0)
-        g_int(0, 1)
-        gf_pe(1, 1, 0)
-        gf_pe(1, 1, 1)
-        load_x(0)
-        gf_sum(1, 0, 0)
-        wv_out(1, 1, 1, 's')
+        feat_mm(0, 1, 0)
+        load_wv(1, 1)
+        feat_mm(0, 1, 1)
+        feat_mm(0, 1, 2)
+        wv_out(0, 1, 1, 's')
+        wv_out(0, 0, 1, 's')
+        feat_mm(0, 1, 3)
+        do_int(1, 1, 'v')
+        feat_out(0, 1, 0, 's')
+        feat_out(0, 1, 1, 's')
+        turn(0, 1, 0)
+        feat_out(0, 1, 2, 's')
+        feat_out(0, 1, 3, 's')
         g_quant(0, 0)
-        do_int(1, 1, 's')
-        gf_sum(1, 0, 1)
-        g_quant(0, 1)
-        do_quant(1, 0)
-        x_int(1, 1, 's')
+        turn_out(0, 1, 0, 's')
+        g_int(0, 1)
+        load_att(1, 0)
+        turn(0, 1, 1)
+        turn_out(0, 1, 1, 's')
+        gf_pe(1, 0, 0)
         gf_pe(1, 0, 2)
+        wv_quant(0, 1)
+        wv_turn(1, 0, 0)
+        wv_turn(1, 0, 1)
+        gf_pe(1, 0, 1)
+        load_att2(1, 0)
+        wv_quant(0, 0)
+        out0_mm(0, 0, 0, 0)
+        load_x(1)
+        do_int(1, 0, 's')
+        g_quant(0, 1)
+        gf_sum(1, 0, 0)
+        wv_out(1, 0, 0, 's')
+        do_quant(1, 0)
+        wv_out(1, 0, 1, 's')
+        load_att(1, 1)
+        out0_mm(0, 3, 0, 0)
+        out0_mm(0, 3, 0, 1)
+        out0_ev(0, 3, 0, 's')
+        gf_sum(1, 0, 1)
+        wv_quant(1, 0)
+        gf_pe(1, 0, 3)
         gf_sum(1, 0, 2)
         gf_sum(1, 0, 3)
-        gf_sum(1, 1, 0)
-        turn_out(0, 0, 0, 's')
-        gf_pe(1, 1, 3)
-        out0_mm(0, 0, 0)
-        out0_ev(0, 0, 0, 's')
-        out0_mm(0, 1, 0)
+        out0_mm(0, 0, 0, 1)
+        out0_ev(0, 0, 0, 'v')
+        x_int(1, 1, 's')
+        wv_turn(1, 1, 0)
+        wv_turn(1, 1, 1)
+        wv_out(1, 1, 0, 's')
         gf_pe(1, 1, 2)
-        gf_sum(1, 1, 1)
-        wv_quant(1, 1)
-        out0_mm(0, 0, 1)
-        turn(0, 1, 0)
-        turn(0, 1, 1)
+        gf_pe(1, 1, 0)
+        load_att2(1, 1)
+        x_int(1, 0, 's')
+        gf_pe(1, 1, 1)
         gf_quant(1, 0)
         feat_mm(1, 0, 0)
-        feat_mm(1, 0, 1)
-        gf_sum(1, 1, 2)
-        gf_sum(1, 1, 3)
-        out0_ev(0, 1, 0, 's')
-        do_quant(1, 1)
-        x_int(0, 0, 's')
-        turn_out(0, 1, 0, 'v')
-        out0_ev(0, 0, 1, 's')
-        gf_quant(1, 1)
-        out0_st(0, 0)
-        feat_out(1, 0, 0, 's')
-        feat_mm(1, 0, 2)
-        feat_out(1, 0, 1, 'v')
-        out0_mm(0, 1, 1)
-        out0_ev(0, 1, 1, 'v')
-        feat_mm(1, 0, 3)
-        x_quant(0, 0)
-        feat_out(1, 0, 2, 'v')
-        feat_out(1, 0, 3, 'v')
+        x_quant(1, 1)
+        wv_out(1, 1, 1, 's')
+        gf_sum(1, 1, 0)
         turn(0, 0, 1)
-        turn_out(0, 1, 1, 's')
-        t_quant(0, 1)
+        turn_out(0, 0, 1, 's')
+        gf_pe(1, 1, 3)
+        out0_mm(0, 3, 1, 0)
+        gf_sum(1, 1, 1)
+        feat_mm(1, 0, 1)
+        feat_mm(1, 0, 2)
+        load_x(0)
+        gf_sum(1, 1, 2)
+        feat_out(1, 0, 0, 's')
+        wv_quant(1, 1)
+        out0_mm(0, 3, 1, 1)
+        feat_out(1, 0, 1, 's')
+        out0_ev(0, 3, 1, 's')
+        out0_st(0, 3)
+        out0_mm(0, 0, 1, 0)
+        out0_mm(0, 0, 1, 1)
+        feat_out(1, 0, 2, 's')
+        out0_mm(0, 1, 1, 0)
+        feat_mm(1, 0, 3)
+        out0_ev(0, 0, 1, 's')
+        out0_mm(0, 1, 0, 0)
+        out0_mm(0, 1, 0, 1)
+        feat_out(1, 0, 3, 's')
+        gf_sum(1, 1, 3)
+        out0_mm(0, 1, 1, 1)
+        do_quant(1, 1)
+        out0_ev(0, 1, 0, 's')
+        out0_ev(0, 1, 1, 's')
+        turn(1, 0, 0)
+        turn(1, 0, 1)
+        turn_out(1, 0, 0, 's')
+        turn_out(1, 0, 1, 's')
+        gf_quant(1, 1)
         feat_mm(1, 1, 0)
         feat_mm(1, 1, 1)
-        out0_mm(0, 3, 0)
-        out0_ev(0, 3, 0, 'v')
-        feat_out(1, 1, 0, 's')
-        turn_out(0, 0, 1, 's')
-        turn(1, 0, 0)
-        x_int(1, 0, 's')
-        feat_out(1, 1, 1, 's')
-        out0_mm(0, 2, 0)
         feat_mm(1, 1, 2)
-        turn_out(1, 0, 0, 's')
-        turn(1, 0, 1)
-        t_quant(0, 0)
-        turn_out(1, 0, 1, 'v')
         feat_mm(1, 1, 3)
-        out0_mm(0, 3, 1)
-        feat_out(1, 1, 2, 's')
-        x_quant(1, 0)
-        feat_out(1, 1, 3, 'v')
-        t_quant(1, 0)
-        out0_mm(0, 2, 1)
-        turn(1, 1, 0)
-        turn_out(1, 1, 0, 'v')
-        out0_ev(0, 3, 1, 's')
-        out0_ev(0, 2, 0, 's')
-        turn(1, 1, 1)
+        out0_st(0, 0)
+        t_quant(0, 0)
+        out0_mm(0, 2, 0, 0)
+        out0_mm(0, 2, 1, 0)
+        x_int(0, 1, 'v')
         out0_st(0, 1)
-        out0_st(0, 3)
-        x_quant(1, 1)
+        t_quant(0, 1)
+        out0_mm(0, 2, 1, 1)
+        feat_out(1, 1, 0, 's')
+        feat_out(1, 1, 1, 'v')
+        x_quant(0, 1)
+        x_int(0, 0, 'v')
+        feat_out(1, 1, 2, 's')
+        out0_mm(0, 2, 0, 1)
+        t_quant(1, 0)
+        feat_out(1, 1, 3, 's')
+        turn(1, 1, 0)
+        turn(1, 1, 1)
+        out1_mm(4, 0, 0)
+        out1_mm(4, 0, 1)
+        out1_mm(7, 0, 0)
+        turn_out(1, 1, 0, 's')
         turn_out(1, 1, 1, 's')
+        out0_ev(0, 2, 0, 'v')
         out0_ev(0, 2, 1, 's')
         out0_st(0, 2)
-        out1_mm(3, 0)
-        out1_mm(2, 0)
+        out1_ev(4, 0, 's')
+        out1_mm(7, 1, 0)
+        out1_mm(4, 1, 0)
         t_quant(1, 1)
-        x_int(0, 1, 'v')
-        x_quant(0, 1)
-        out1_mm(2, 1)
+        out1_mm(4, 1, 1)
+        out1_ev(4, 1, 's')
+        out1_mm(6, 0, 0)
+        out1_mm(7, 0, 1)
+        out1_ev(7, 0, 's')
+        x_quant(0, 0)
+        out1_mm(0, 0, 0)
+        out1_mm(7, 1, 1)
+        out1_ev(7, 1, 's')
+        out1_mm(6, 0, 1)
+        out1_ev(6, 0, 's')
+        out1_mm(6, 1, 0)
+        out1_st(4)
+        out1_mm(6, 1, 1)
+        out1_ev(6, 1, 's')
+        x_quant(1, 0)
+        out1_mm(0, 0, 1)
+        out1_mm(0, 1, 0)
+        out1_mm(0, 1, 1)
+        out1_st(7)
+        g_int(1, 0)
+        out1_ev(0, 0, 's')
+        g_int(1, 1)
+        out1_mm(5, 0, 0)
+        out1_st(6)
+        out1_mm(2, 0, 0)
+        out1_mm(2, 0, 1)
+        out1_ev(0, 1, 's')
+        out1_st(0)
+        out1_mm(5, 1, 0)
+        out1_mm(2, 1, 0)
+        out1_mm(2, 1, 1)
         out1_ev(2, 0, 's')
         out1_ev(2, 1, 's')
-        out1_st(2)
-        g_int(1, 0)
-        g_int(1, 1)
-        out1_mm(3, 1)
-        out1_mm(0, 1)
-        out1_ev(3, 0, 's')
-        out1_ev(3, 1, 's')
-        out1_mm(0, 0)
-        out1_ev(0, 0, 's')
-        out1_ev(0, 1, 's')
-        out1_mm(7, 0)
-        out1_ev(7, 0, 's')
-        out1_mm(7, 1)
         g_quant(1, 0)
-        out1_st(3)
-        out1_ev(7, 1, 's')
-        out1_mm(4, 0)
-        out1_ev(4, 0, 's')
-        out1_mm(4, 1)
-        out1_mm(6, 0)
-        out1_ev(4, 1, 's')
-        out1_ev(6, 0, 's')
-        out1_st(0)
-        out1_st(7)
-        out1_mm(6, 1)
-        out1_ev(6, 1, 's')
+        out0_mm(1, 0, 0, 0)
+        out1_mm(5, 0, 1)
+        out1_st(2)
+        out1_ev(5, 0, 's')
         g_quant(1, 1)
-        out0_mm(1, 0, 0)
-        out0_mm(1, 3, 1)
-        out1_st(4)
+        out0_mm(1, 0, 0, 1)
+        out1_mm(5, 1, 1)
+        out0_mm(1, 2, 1, 0)
+        out0_mm(1, 2, 1, 1)
+        out1_ev(5, 1, 'v')
+        out1_st(5)
         out0_ev(1, 0, 0, 's')
-        out0_mm(1, 0, 1)
-        out0_ev(1, 0, 1, 'v')
-        out0_mm(1, 1, 1)
-        out1_st(6)
-        out0_st(1, 0)
-        out0_mm(1, 3, 0)
-        out0_ev(1, 3, 0, 'v')
-        out0_ev(1, 3, 1, 's')
-        out0_st(1, 3)
-        out1_mm(1, 0)
-        out1_ev(1, 0, 's')
-        out1_mm(1, 1)
-        out1_ev(1, 1, 's')
-        out0_mm(1, 1, 0)
-        out0_ev(1, 1, 0, 's')
-        out0_ev(1, 1, 1, 'v')
-        out0_mm(1, 2, 0)
+        out0_mm(1, 2, 0, 0)
+        out0_mm(1, 2, 0, 1)
+        out0_mm(1, 1, 0, 0)
+        out0_mm(1, 1, 0, 1)
+        out0_mm(1, 0, 1, 0)
         out0_ev(1, 2, 0, 's')
-        out0_mm(1, 2, 1)
-        out1_mm(5, 1)
-        out1_st(1)
-        out0_st(1, 1)
         out0_ev(1, 2, 1, 'v')
         out0_st(1, 2)
-        out1_mm(5, 0)
-        out1_ev(5, 0, 's')
-        out1_ev(5, 1, 's')
-        out1_st(5)
+        out0_mm(1, 0, 1, 1)
+        out0_ev(1, 0, 1, 's')
+        out0_mm(1, 3, 1, 0)
+        out0_mm(1, 1, 1, 0)
+        out0_mm(1, 1, 1, 1)
+        out1_mm(3, 0, 0)
+        out0_st(1, 0)
+        out1_mm(3, 1, 0)
+        out1_mm(3, 1, 1)
+        out0_ev(1, 1, 0, 's')
+        out0_ev(1, 1, 1, 's')
+        out1_mm(3, 0, 1)
+        out0_st(1, 1)
+        out0_mm(1, 3, 1, 1)
+        out1_ev(3, 0, 'v')
+        out1_ev(3, 1, 's')
+        out1_st(3)
+        out1_mm(1, 1, 0)
+        out0_mm(1, 3, 0, 0)
+        out0_mm(1, 3, 0, 1)
+        out0_ev(1, 3, 0, 's')
+        out1_mm(1, 0, 0)
+        out1_mm(1, 0, 1)
+        out0_ev(1, 3, 1, 'v')
+        out0_st(1, 3)
+        out1_ev(1, 0, 'v')
+        out1_half(1, 0)
+        out1_mm(1, 1, 1)
+        out1_ev(1, 1, 's')
+        out1_half(1, 1)

@@ -128,10 +128,12 @@ def tile_gfsa_pa_v_kernel(tc, x, att, Wv, bv, w0, w1, wK, att2, grad_out, out_0,
             else:
                 nc.scalar.copy(out=out, in_=in_)
 
-        def do_int(b, h, eng):
+        def do_int(b, h):
             t = stage.tile([P, 2048], BF16, name="do_g", align_bytes=64)
-            copy(eng, t[:].rearrange("p (t m j) -> p m t j", t=PACK, j=PACK),
-                 do_raw[b, h].rearrange("p j (m t) -> p m t j", t=PACK))
+            nc.scalar.copy(
+                out=t[:].rearrange("p (t m j) -> p m t j", t=PACK, j=PACK),
+                in_=do_raw[b, h].rearrange("p j (m t) -> p m t j", t=PACK),
+            )
             do_g[b, h] = t
 
         def do_quant(b, h):
@@ -205,16 +207,16 @@ def tile_gfsa_pa_v_kernel(tc, x, att, Wv, bv, w0, w1, wK, att2, grad_out, out_0,
 
         def feat_out(b, h, t, eng):
             if t == 0:
-                f_sb[b, h] = stage.tile([P, PACK, N], BF16, name="f_sb", align_bytes=64)
-            copy(eng, f_sb[b, h][:, t, :], banks["f", b, h, t][:])
+                f_sb[b, h] = stage.tile([P, PACK, 2, N // 2], BF16, name="f_sb", align_bytes=64)
+            copy(eng, f_sb[b, h][:, t].rearrange("p u (q e) -> p u q e", e=2),
+                 banks["f", b, h, t][:].rearrange("p (q u e) -> p u q e", u=2, e=2))
 
         def turn(b, h, tt):
             bank = pst.tile([P, 2, 2, P], F32, name="tr")
             banks["t", b, h, tt] = bank
             for t2 in range(2):
-                words = f_sb[b, h][:, 2 * tt + t2, :].bitcast(F32)
                 for u in range(2):
-                    nc.tensor.transpose(bank[:, t2, u, :], words[:, u::2], id_f[:])
+                    nc.tensor.transpose(bank[:, t2, u, :], f_sb[b, h][:, 2 * tt + t2, u, :].bitcast(F32), id_f[:])
 
         def turn_out(b, h, tt, eng):
             if tt == 0:
@@ -224,10 +226,11 @@ def tile_gfsa_pa_v_kernel(tc, x, att, Wv, bv, w0, w1, wK, att2, grad_out, out_0,
 
         def g_int(b, h):
             g_g[b, h] = stage.tile([P, 2048], BF16, name="g_g", align_bytes=64)
-            nc.vector.tensor_copy(
-                out=g_g[b, h][:].rearrange("p (c i t) -> p c t i", i=4, t=PACK),
-                in_=f_sb[b, h][:].rearrange("p t (c i) -> p c t i", i=4),
-            )
+            for u in range(2):
+                nc.vector.tensor_copy(
+                    out=g_g[b, h][:].rearrange("p (q u e t) -> p q u t e", u=2, e=2, t=PACK)[:, :, u],
+                    in_=f_sb[b, h][:, :, u, :].rearrange("p t (q e) -> p q t e", e=2),
+                )
 
         def g_quant(b, h):
             g_q[b, h] = codes_tile("g_q%d%d" % (b, h))
@@ -298,269 +301,269 @@ def tile_gfsa_pa_v_kernel(tc, x, att, Wv, bv, w0, w1, wK, att2, grad_out, out_0,
         def out1_half(i, h):
             nc.sync.dma_start(out=out_1[P * i : P * (i + 1), 512 * h : 512 * (h + 1)], in_=ots["o1", i][:, 512 * h : 512 * (h + 1)])
 
-        load_do(0, 0)
-        do_int(0, 0, 'v')
-        do_quant(0, 0)
-        load_w()
         load_att(0, 0)
+        load_w()
         consts(0)
-        consts(1)
-        gf_pe(0, 0, 2)
         load_att2(0, 0)
+        gf_pe(0, 0, 2)
         gf_lin()
-        load_att(0, 1)
-        gf_pe(0, 0, 3)
-        gf_pe(0, 1, 0)
-        load_do(0, 1)
-        do_int(0, 1, 's')
         gf_pe(0, 0, 0)
         gf_pe(0, 0, 1)
         gf_sum(0, 0, 0)
         gf_sum(0, 0, 1)
-        gf_pe(0, 1, 1)
-        gf_pe(0, 1, 2)
         gf_sum(0, 0, 2)
+        gf_pe(0, 0, 3)
         gf_sum(0, 0, 3)
+        consts(1)
+        load_do(0, 0)
+        do_int(0, 0)
+        load_wv(0, 0)
+        wv_turn(0, 0, 0)
+        wv_turn(0, 1, 0)
+        load_att(0, 1)
+        gf_pe(0, 1, 0)
+        do_quant(0, 0)
+        load_att2(0, 1)
+        wv_out(0, 0, 0, 's')
+        gf_pe(0, 1, 1)
+        load_do(0, 1)
         gf_quant(0, 0)
         feat_mm(0, 0, 0)
         feat_mm(0, 0, 1)
-        load_wv(0, 0)
-        wv_turn(0, 0, 0)
-        wv_out(0, 0, 0, 's')
         feat_mm(0, 0, 2)
-        wv_turn(0, 1, 0)
-        feat_out(0, 0, 0, 'v')
-        load_att2(0, 1)
-        do_quant(0, 1)
+        feat_out(0, 0, 0, 's')
+        gf_pe(0, 1, 2)
         feat_out(0, 0, 1, 's')
-        turn(0, 0, 0)
-        load_wv(1, 0)
-        gf_pe(0, 1, 3)
-        wv_out(0, 1, 0, 's')
+        wv_out(0, 1, 0, 'v')
+        do_int(0, 1)
         gf_sum(0, 1, 0)
-        feat_out(0, 0, 2, 's')
-        load_wv(0, 1)
-        feat_mm(0, 0, 3)
-        wv_turn(0, 1, 1)
-        turn_out(0, 0, 0, 's')
-        wv_turn(0, 0, 1)
         gf_sum(0, 1, 1)
+        load_wv(0, 1)
+        gf_pe(0, 1, 3)
         gf_sum(0, 1, 2)
         gf_sum(0, 1, 3)
+        feat_out(0, 0, 2, 's')
         gf_quant(0, 1)
-        load_do_both(1)
-        feat_out(0, 0, 3, 's')
-        g_int(0, 0)
+        wv_turn(0, 1, 1)
+        wv_out(0, 1, 1, 's')
+        do_quant(0, 1)
+        wv_turn(0, 0, 1)
+        feat_mm(0, 0, 3)
         feat_mm(0, 1, 0)
-        load_wv(1, 1)
+        wv_out(0, 0, 1, 's')
         feat_mm(0, 1, 1)
         feat_mm(0, 1, 2)
-        wv_out(0, 1, 1, 's')
-        wv_out(0, 0, 1, 's')
-        feat_mm(0, 1, 3)
-        do_int(1, 1, 'v')
-        feat_out(0, 1, 0, 's')
-        feat_out(0, 1, 1, 's')
-        turn(0, 1, 0)
-        feat_out(0, 1, 2, 's')
-        feat_out(0, 1, 3, 's')
-        g_quant(0, 0)
-        turn_out(0, 1, 0, 's')
-        g_int(0, 1)
-        load_att(1, 0)
-        turn(0, 1, 1)
-        turn_out(0, 1, 1, 's')
-        gf_pe(1, 0, 0)
-        gf_pe(1, 0, 2)
-        wv_quant(0, 1)
-        wv_turn(1, 0, 0)
-        wv_turn(1, 0, 1)
-        gf_pe(1, 0, 1)
-        load_att2(1, 0)
-        wv_quant(0, 0)
-        out0_mm(0, 0, 0, 0)
-        load_x(1)
-        do_int(1, 0, 's')
-        g_quant(0, 1)
-        gf_sum(1, 0, 0)
-        wv_out(1, 0, 0, 's')
-        do_quant(1, 0)
-        wv_out(1, 0, 1, 's')
         load_att(1, 1)
-        out0_mm(0, 3, 0, 0)
-        out0_mm(0, 3, 0, 1)
-        out0_ev(0, 3, 0, 's')
-        gf_sum(1, 0, 1)
-        wv_quant(1, 0)
-        gf_pe(1, 0, 3)
-        gf_sum(1, 0, 2)
-        gf_sum(1, 0, 3)
-        out0_mm(0, 0, 0, 1)
-        out0_ev(0, 0, 0, 'v')
-        x_int(1, 1, 's')
-        wv_turn(1, 1, 0)
-        wv_turn(1, 1, 1)
-        wv_out(1, 1, 0, 's')
-        gf_pe(1, 1, 2)
-        gf_pe(1, 1, 0)
+        load_do_both(1)
+        feat_out(0, 0, 3, 'v')
+        feat_out(0, 1, 0, 'v')
+        feat_out(0, 1, 1, 's')
+        feat_out(0, 1, 2, 's')
+        feat_mm(0, 1, 3)
+        feat_out(0, 1, 3, 's')
+        turn(0, 0, 0)
         load_att2(1, 1)
-        x_int(1, 0, 's')
+        turn(0, 1, 0)
+        turn_out(0, 1, 0, 's')
         gf_pe(1, 1, 1)
-        gf_quant(1, 0)
-        feat_mm(1, 0, 0)
-        x_quant(1, 1)
-        wv_out(1, 1, 1, 's')
-        gf_sum(1, 1, 0)
-        turn(0, 0, 1)
-        turn_out(0, 0, 1, 's')
+        g_int(0, 0)
+        gf_pe(1, 1, 0)
         gf_pe(1, 1, 3)
-        out0_mm(0, 3, 1, 0)
+        wv_quant(0, 0)
+        g_int(0, 1)
+        turn_out(0, 0, 0, 's')
+        load_wv(1, 0)
+        gf_sum(1, 1, 0)
         gf_sum(1, 1, 1)
-        feat_mm(1, 0, 1)
-        feat_mm(1, 0, 2)
-        load_x(0)
+        gf_pe(1, 1, 2)
+        load_att(1, 0)
+        gf_pe(1, 0, 0)
         gf_sum(1, 1, 2)
-        feat_out(1, 0, 0, 's')
-        wv_quant(1, 1)
-        out0_mm(0, 3, 1, 1)
-        feat_out(1, 0, 1, 's')
-        out0_ev(0, 3, 1, 's')
-        out0_st(0, 3)
-        out0_mm(0, 0, 1, 0)
-        out0_mm(0, 0, 1, 1)
-        feat_out(1, 0, 2, 's')
-        out0_mm(0, 1, 1, 0)
-        feat_mm(1, 0, 3)
-        out0_ev(0, 0, 1, 's')
-        out0_mm(0, 1, 0, 0)
-        out0_mm(0, 1, 0, 1)
-        feat_out(1, 0, 3, 's')
         gf_sum(1, 1, 3)
-        out0_mm(0, 1, 1, 1)
-        do_quant(1, 1)
-        out0_ev(0, 1, 0, 's')
-        out0_ev(0, 1, 1, 's')
-        turn(1, 0, 0)
-        turn(1, 0, 1)
-        turn_out(1, 0, 0, 's')
-        turn_out(1, 0, 1, 's')
+        wv_turn(1, 1, 0)
+        do_int(1, 1)
+        gf_pe(1, 0, 1)
+        wv_quant(0, 1)
+        do_int(1, 0)
+        turn(0, 0, 1)
+        wv_out(1, 1, 0, 's')
         gf_quant(1, 1)
+        gf_pe(1, 0, 2)
+        do_quant(1, 1)
         feat_mm(1, 1, 0)
         feat_mm(1, 1, 1)
         feat_mm(1, 1, 2)
-        feat_mm(1, 1, 3)
-        out0_st(0, 0)
-        t_quant(0, 0)
-        out0_mm(0, 2, 0, 0)
-        out0_mm(0, 2, 1, 0)
-        x_int(0, 1, 'v')
-        out0_st(0, 1)
-        t_quant(0, 1)
-        out0_mm(0, 2, 1, 1)
+        turn_out(0, 0, 1, 's')
+        load_wv(1, 1)
+        g_quant(0, 1)
         feat_out(1, 1, 0, 's')
-        feat_out(1, 1, 1, 'v')
-        x_quant(0, 1)
-        x_int(0, 0, 'v')
+        feat_out(1, 1, 1, 's')
+        wv_turn(1, 1, 1)
+        g_quant(0, 0)
         feat_out(1, 1, 2, 's')
+        load_att2(1, 0)
+        gf_sum(1, 0, 0)
+        load_x(1)
+        gf_pe(1, 0, 3)
+        gf_sum(1, 0, 1)
+        gf_sum(1, 0, 2)
+        gf_sum(1, 0, 3)
+        wv_turn(1, 0, 0)
+        wv_out(1, 1, 1, 's')
+        wv_turn(1, 0, 1)
+        wv_out(1, 0, 0, 'v')
+        do_quant(1, 0)
+        feat_mm(1, 1, 3)
+        out0_mm(0, 2, 0, 0)
         out0_mm(0, 2, 0, 1)
-        t_quant(1, 0)
-        feat_out(1, 1, 3, 's')
+        x_int(1, 1, 's')
+        gf_quant(1, 0)
+        turn(0, 1, 1)
+        wv_out(1, 0, 1, 's')
+        feat_mm(1, 0, 0)
+        wv_quant(1, 1)
+        turn_out(0, 1, 1, 'v')
+        out0_ev(0, 2, 0, 's')
+        feat_mm(1, 0, 1)
+        feat_mm(1, 0, 2)
         turn(1, 1, 0)
-        turn(1, 1, 1)
-        out1_mm(4, 0, 0)
-        out1_mm(4, 0, 1)
-        out1_mm(7, 0, 0)
-        turn_out(1, 1, 0, 's')
-        turn_out(1, 1, 1, 's')
-        out0_ev(0, 2, 0, 'v')
+        wv_quant(1, 0)
+        feat_mm(1, 0, 3)
+        t_quant(0, 1)
+        out0_mm(0, 2, 1, 0)
+        out0_mm(0, 0, 1, 0)
+        feat_out(1, 1, 3, 's')
+        feat_out(1, 0, 0, 's')
+        feat_out(1, 0, 1, 's')
+        out0_mm(0, 2, 1, 1)
+        t_quant(0, 0)
+        out0_mm(0, 3, 0, 0)
+        feat_out(1, 0, 2, 's')
+        feat_out(1, 0, 3, 's')
+        out0_mm(0, 0, 0, 0)
+        out0_mm(0, 0, 0, 1)
+        load_x(0)
+        out0_mm(0, 0, 1, 1)
+        x_int(0, 1, 'v')
+        out0_mm(0, 3, 1, 0)
         out0_ev(0, 2, 1, 's')
-        out0_st(0, 2)
-        out1_ev(4, 0, 's')
-        out1_mm(7, 1, 0)
-        out1_mm(4, 1, 0)
-        t_quant(1, 1)
-        out1_mm(4, 1, 1)
-        out1_ev(4, 1, 's')
-        out1_mm(6, 0, 0)
-        out1_mm(7, 0, 1)
-        out1_ev(7, 0, 's')
-        x_quant(0, 0)
-        out1_mm(0, 0, 0)
-        out1_mm(7, 1, 1)
-        out1_ev(7, 1, 's')
-        out1_mm(6, 0, 1)
-        out1_ev(6, 0, 's')
-        out1_mm(6, 1, 0)
-        out1_st(4)
-        out1_mm(6, 1, 1)
-        out1_ev(6, 1, 's')
-        x_quant(1, 0)
-        out1_mm(0, 0, 1)
-        out1_mm(0, 1, 0)
-        out1_mm(0, 1, 1)
-        out1_st(7)
+        out0_mm(0, 1, 1, 0)
         g_int(1, 0)
-        out1_ev(0, 0, 's')
+        turn_out(1, 1, 0, 's')
         g_int(1, 1)
-        out1_mm(5, 0, 0)
-        out1_st(6)
-        out1_mm(2, 0, 0)
-        out1_mm(2, 0, 1)
-        out1_ev(0, 1, 's')
-        out1_st(0)
-        out1_mm(5, 1, 0)
-        out1_mm(2, 1, 0)
-        out1_mm(2, 1, 1)
-        out1_ev(2, 0, 's')
-        out1_ev(2, 1, 's')
+        out0_mm(0, 3, 0, 1)
+        out0_mm(0, 1, 1, 1)
+        out0_mm(0, 1, 0, 0)
+        out0_mm(0, 1, 0, 1)
+        out0_ev(0, 0, 0, 's')
+        out0_ev(0, 0, 1, 's')
+        out0_ev(0, 1, 0, 'v')
+        out0_ev(0, 3, 0, 's')
+        turn(1, 1, 1)
+        turn(1, 0, 0)
+        turn(1, 0, 1)
+        out0_mm(0, 3, 1, 1)
         g_quant(1, 0)
-        out0_mm(1, 0, 0, 0)
-        out1_mm(5, 0, 1)
-        out1_st(2)
-        out1_ev(5, 0, 's')
-        g_quant(1, 1)
-        out0_mm(1, 0, 0, 1)
-        out1_mm(5, 1, 1)
-        out0_mm(1, 2, 1, 0)
-        out0_mm(1, 2, 1, 1)
-        out1_ev(5, 1, 'v')
-        out1_st(5)
-        out0_ev(1, 0, 0, 's')
-        out0_mm(1, 2, 0, 0)
-        out0_mm(1, 2, 0, 1)
         out0_mm(1, 1, 0, 0)
+        g_quant(1, 1)
         out0_mm(1, 1, 0, 1)
-        out0_mm(1, 0, 1, 0)
-        out0_ev(1, 2, 0, 's')
-        out0_ev(1, 2, 1, 'v')
-        out0_st(1, 2)
-        out0_mm(1, 0, 1, 1)
-        out0_ev(1, 0, 1, 's')
-        out0_mm(1, 3, 1, 0)
+        out0_ev(0, 1, 1, 's')
+        turn_out(1, 1, 1, 's')
+        out0_mm(1, 3, 0, 0)
+        out0_ev(0, 3, 1, 'v')
+        x_int(1, 0, 's')
+        x_quant(0, 1)
         out0_mm(1, 1, 1, 0)
         out0_mm(1, 1, 1, 1)
-        out1_mm(3, 0, 0)
-        out0_st(1, 0)
-        out1_mm(3, 1, 0)
-        out1_mm(3, 1, 1)
         out0_ev(1, 1, 0, 's')
         out0_ev(1, 1, 1, 's')
-        out1_mm(3, 0, 1)
-        out0_st(1, 1)
-        out0_mm(1, 3, 1, 1)
-        out1_ev(3, 0, 'v')
-        out1_ev(3, 1, 's')
-        out1_st(3)
-        out1_mm(1, 1, 0)
-        out0_mm(1, 3, 0, 0)
         out0_mm(1, 3, 0, 1)
+        x_quant(1, 1)
+        out1_mm(6, 1, 0)
+        t_quant(1, 1)
+        out1_mm(6, 0, 0)
+        out1_mm(6, 1, 1)
+        out0_st(0, 2)
+        out0_st(0, 0)
+        out0_mm(1, 3, 1, 0)
+        out0_mm(1, 3, 1, 1)
+        turn_out(1, 0, 0, 's')
+        turn_out(1, 0, 1, 's')
+        x_int(0, 0, 'v')
+        out0_st(0, 1)
+        out1_mm(4, 1, 0)
+        out1_mm(4, 1, 1)
         out0_ev(1, 3, 0, 's')
+        out0_ev(1, 3, 1, 's')
+        out1_mm(4, 0, 0)
+        t_quant(1, 0)
+        out1_mm(6, 0, 1)
+        out1_mm(4, 0, 1)
+        x_quant(0, 0)
         out1_mm(1, 0, 0)
-        out1_mm(1, 0, 1)
-        out0_ev(1, 3, 1, 'v')
+        out1_ev(6, 0, 'v')
+        out1_mm(0, 0, 0)
+        out1_mm(0, 1, 0)
+        out1_ev(6, 1, 's')
+        x_quant(1, 0)
+        out1_ev(4, 0, 's')
+        out1_ev(4, 1, 's')
+        out0_st(0, 3)
+        out0_st(1, 1)
+        out1_mm(2, 0, 0)
+        out1_mm(0, 0, 1)
+        out1_ev(0, 0, 'v')
+        out1_mm(0, 1, 1)
+        out1_ev(0, 1, 'v')
         out0_st(1, 3)
-        out1_ev(1, 0, 'v')
-        out1_half(1, 0)
+        out1_mm(1, 0, 1)
+        out1_mm(2, 0, 1)
+        out1_mm(3, 0, 0)
+        out1_mm(3, 0, 1)
+        out1_mm(2, 1, 0)
+        out1_mm(1, 1, 0)
         out1_mm(1, 1, 1)
+        out1_mm(3, 1, 0)
+        out1_ev(1, 0, 's')
+        out1_st(6)
+        out1_ev(2, 0, 'v')
+        out1_mm(2, 1, 1)
+        out1_st(4)
+        out1_ev(2, 1, 'v')
         out1_ev(1, 1, 's')
+        out1_st(0)
+        out1_half(1, 0)
+        out0_mm(1, 2, 0, 0)
         out1_half(1, 1)
+        out1_ev(3, 0, 'v')
+        out1_mm(5, 0, 0)
+        out1_mm(5, 0, 1)
+        out1_mm(3, 1, 1)
+        out0_mm(1, 2, 0, 1)
+        out1_ev(3, 1, 's')
+        out1_st(2)
+        out0_mm(1, 2, 1, 0)
+        out0_mm(1, 2, 1, 1)
+        out0_ev(1, 2, 0, 's')
+        out0_mm(1, 0, 0, 0)
+        out0_mm(1, 0, 0, 1)
+        out0_ev(1, 0, 0, 's')
+        out0_mm(1, 0, 1, 0)
+        out0_mm(1, 0, 1, 1)
+        out0_ev(1, 2, 1, 'v')
+        out1_st(3)
+        out0_st(1, 2)
+        out1_mm(5, 1, 0)
+        out0_ev(1, 0, 1, 'v')
+        out1_mm(5, 1, 1)
+        out1_ev(5, 0, 's')
+        out0_st(1, 0)
+        out1_ev(5, 1, 's')
+        out1_mm(7, 1, 0)
+        out1_st(5)
+        out1_mm(7, 0, 0)
+        out1_mm(7, 0, 1)
+        out1_ev(7, 0, 'v')
+        out1_mm(7, 1, 1)
+        out1_ev(7, 1, 'v')
+        out1_st(7)

from contextlib import ExitStack

import concourse.mybir as mybir
from concourse.masks import make_identity

B, H, N, D, E = 2, 2, 512, 1024, 1024
DH = 512
P = 128
PACK = 4
F32 = mybir.dt.float32
BF16 = mybir.dt.bfloat16
U32 = mybir.dt.uint32
U8 = mybir.dt.uint8
E4M3 = mybir.dt.float8_e4m3fn_x4
E5M2 = mybir.dt.float8_e5m2_x4
ALU = mybir.AluOpType

FLOPS = 2 * (B * H * N * N * DH) + 2 * 2 * (B * N * E * D)


def tile_gfsa_pa_v_kernel(tc, x, att, Wv, bv, w0, w1, wK, att2, grad_out, out_0, out_1):
    nc = tc.nc
    with ExitStack() as ctx:
        const = ctx.enter_context(tc.tile_pool(name="const", bufs=1))
        raw = ctx.enter_context(tc.tile_pool(name="raw", bufs=1))
        stage = ctx.enter_context(tc.tile_pool(name="stage", bufs=2))
        keep = ctx.enter_context(tc.tile_pool(name="keep", bufs=1))
        outs = ctx.enter_context(tc.tile_pool(name="outs", bufs=6))
        pst = ctx.enter_context(tc.psum_pool(name="pst", bufs=2))
        psm = ctx.enter_context(tc.psum_pool(name="psm", bufs=6))
        ctx.enter_context(tc.manual_schedule())

        wt = {}

        def load_w():
            for nm, src in (("w0", w0), ("w1", w1), ("wK", wK)):
                t = const.tile([P, H], BF16, name="wt_" + nm)
                nc.sync.dma_start(out=t[:], in_=src.partition_broadcast(P))
                wt[nm] = t

        do_raw = {}
        att_sb = {}
        att2_sb = {}
        x_raw = {}

        def load_do(b, h):
            t = raw.tile([P, PACK, DH], BF16, name="do_raw%d%d" % (b, h))
            nc.sync.dma_start(out=t[:], in_=grad_out[b, :, DH * h : DH * (h + 1)].rearrange("(p j) e -> p j e", j=PACK))
            do_raw[b, h] = t[:]

        def load_do_both(b):
            t = raw.tile([P, PACK, E], BF16, name="do_raw%d" % b)
            nc.sync.dma_start(out=t[:], in_=grad_out[b].rearrange("(p j) e -> p j e", j=PACK))
            for h in range(H):
                do_raw[b, h] = t[:, :, DH * h : DH * (h + 1)]

        def load_att(b, h):
            t = raw.tile([P, PACK, N], BF16, name="att_sb", bufs=3)
            nc.sync.dma_start(out=t[:], in_=att[b, h].rearrange("(p j) k -> p j k", j=PACK))
            att_sb[b, h] = t

        def load_att2(b, h):
            t = raw.tile([P, PACK, N], F32, name="att2_sb", bufs=3)
            nc.sync.dma_start(out=t[:], in_=att2[b, h].rearrange("(p j) k -> p j k", j=PACK))
            att2_sb[b, h] = t

        def load_x(b):
            t = raw.tile([P, PACK, D], BF16, name="x_raw%d" % b)
            nc.sync.dma_start(out=t[:], in_=x[b].rearrange("(p j) d -> p j d", j=PACK))
            x_raw[b] = t

        wv_raw = {}

        def load_wv(i0, ii):
            t = raw.tile([P, 2, E], BF16, name="wv_raw%d%d" % (i0, ii))
            r = 512 * i0 + 256 * ii
            nc.sync.dma_start(out=t[:], in_=Wv[r : r + 256, :].rearrange("(i p) e -> p i e", p=P))
            wv_raw[i0, ii] = t

        id_bf = const.tile([P, P], BF16)
        make_identity(nc, id_bf[:])
        id_f = const.tile([P, P], F32)
        make_identity(nc, id_f[:])
        irep = const.tile([P, PACK, P], BF16)
        for j in range(PACK):
            nc.vector.tensor_copy(out=irep[:, j, :], in_=id_bf[:])
        diag = {}
        wk2 = const.tile([P, H], F32)
        c1 = const.tile([P, H], F32)
        w0f = const.tile([P, H], F32)
        KD = 256
        dmask = const.tile([P, PACK * (KD + 1)], F32)
        nc.gpsimd.memset(dmask[:], 0.0)

        def consts(h):
            for nm, sgn in (("w1", 1.0), ("wK", -1.0), ("w0", 1.0)):
                t = const.tile([P, P], BF16, name="diag_%s%d" % (nm, h))
                nc.gpsimd.tensor_scalar(out=t[:], in0=id_bf[:], scalar1=wt[nm][:, h : h + 1], scalar2=sgn, op0=ALU.mult, op1=ALU.mult)
                diag[nm, h] = t
            if h == 0:
                nc.gpsimd.tensor_scalar(out=wk2[:], in0=wt["wK"][:], scalar1=2.0, scalar2=0.0, op0=ALU.mult, op1=ALU.add)
                nc.gpsimd.tensor_tensor(out=c1[:], in0=wt["w1"][:], in1=wt["wK"][:], op=ALU.subtract)
                nc.gpsimd.tensor_copy(out=w0f[:], in_=wt["w0"][:])
                nc.gpsimd.tensor_scalar(
                    out=dmask[:].rearrange("p (j x) -> p j x", x=KD + 1)[:, :, 0:KD:PACK],
                    in0=irep[:, :, 0 : KD // PACK],
                    scalar1=w0f[:, 0:1],
                    scalar2=0.0,
                    op0=ALU.mult,
                    op1=ALU.add,
                )

        def codes_tile(name, bufs=1):
            c = keep.tile([P, 512], U32, name=name + "_c", align_bytes=64, bufs=bufs)
            s = keep.tile([P, 512], U8, name=name + "_s", align_bytes=64, bufs=bufs)
            return c, s

        def quant(cs, src, fmt):
            c, s = cs
            nc.vector.quantize_mx(out=c[:].bitcast(fmt), scales=s[:], in_=src[:])

        do_g, do_q, gf_g, gf_q, f_sb, g_g, g_q, t_g, t_q = {}, {}, {}, {}, {}, {}, {}, {}, {}
        wv_g, wv_q, x_g, x_q = {}, {}, {}, {}

        def copy(eng, out, in_):
            if eng == "v":
                nc.vector.tensor_copy(out=out, in_=in_)
            else:
                nc.scalar.copy(out=out, in_=in_)

        def do_int(b, h):
            t = stage.tile([P, 2048], BF16, name="do_g", align_bytes=64)
            nc.scalar.copy(
                out=t[:].rearrange("p (t m j) -> p m t j", t=PACK, j=PACK),
                in_=do_raw[b, h].rearrange("p j (m t) -> p m t j", t=PACK),
            )
            do_g[b, h] = t

        def do_quant(b, h):
            do_q[b, h] = codes_tile("do_q", 2)
            quant(do_q[b, h], do_g[b, h], E5M2)

        lin00 = stage.tile([P, PACK, KD], F32, name="lin00", bufs=1)

        def gf_lin():
            nc.vector.scalar_tensor_tensor(
                out=lin00[:],
                in0=att_sb[0, 0][:, :, 0:KD],
                scalar=c1[:, 0:1],
                in1=dmask[:, 0 : PACK * KD].rearrange("p (j k) -> p j k", j=PACK),
                op0=ALU.mult,
                op1=ALU.add,
            )

        lins = {}

        def gf_pe(b, h, kb):
            ks = slice(P * kb, P * (kb + 1))
            if (b, h) == (0, 0) and kb < KD // P:
                lins[b, h, kb] = lin00[:, :, ks].rearrange("p j k -> p k j")
            else:
                bank = psm.tile([P, 512], F32, name="mm")
                bj = bank[:].rearrange("p (j k) -> p j k", j=PACK)
                rhs = att_sb[b, h][:, :, ks]
                nc.tensor.matmul(out=bj, lhsT=diag["w1", h][:], rhs=rhs, start=True, stop=False)
                ms = slice(32 * kb, 32 * (kb + 1))
                nc.tensor.matmul(
                    out=bank[:, 0:387].rearrange("p (j x) -> p j x", x=129)[:, :, 0:125:4],
                    lhsT=diag["w0", h][:], rhs=irep[:, 0:3, ms], start=False, stop=False)
                nc.tensor.matmul(out=bank[:, 387:512:4], lhsT=diag["w0", h][:], rhs=irep[:, 3, ms], start=False, stop=False)
                nc.tensor.matmul(out=bj, lhsT=diag["wK", h][:], rhs=rhs, start=False, stop=True)
                lins[b, h, kb] = bj.rearrange("p j k -> p k j")

        def gf_sum(b, h, kb):
            if kb == 0:
                gf_g[b, h] = stage.tile([P, 2048], BF16, name="gf_g", align_bytes=64)
            ks = slice(P * kb, P * (kb + 1))
            nc.vector.scalar_tensor_tensor(
                out=gf_g[b, h][:, 512 * kb : 512 * (kb + 1)].rearrange("p (k j) -> p k j", j=PACK),
                in0=att2_sb[b, h][:, :, ks].rearrange("p j k -> p k j"),
                scalar=wk2[:, h : h + 1],
                in1=lins[b, h, kb],
                op0=ALU.mult,
                op1=ALU.add,
            )

        def gf_quant(b, h):
            gf_q[b, h] = codes_tile("gf_q", 2)
            quant(gf_q[b, h], gf_g[b, h], E4M3)

        def mx(out, l, ls, lf, r, rs, rf, cols_l, cols_r, start, stop):
            nc.tensor.matmul_mx(
                out=out, lhsT=l[:, cols_l].bitcast(lf), lhsT_scale=ls[:, cols_l],
                rhs=r[:, cols_r].bitcast(rf), rhs_scale=rs[:, cols_r], start=start, stop=stop)

        banks = {}

        def mm_bank(*k):
            bank = psm.tile([P, 512], F32, name="mm")
            banks[k] = bank
            return bank

        def feat_mm(b, h, t):
            bank = mm_bank("f", b, h, t)
            mx(bank[:], do_q[b, h][0], do_q[b, h][1], E5M2, gf_q[b, h][0], gf_q[b, h][1], E4M3,
               slice(P * t, P * (t + 1)), slice(0, 512), True, True)

        def feat_out(b, h, t, eng):
            if t == 0:
                f_sb[b, h] = stage.tile([P, PACK, 2, N // 2], BF16, name="f_sb", align_bytes=64)
            copy(eng, f_sb[b, h][:, t].rearrange("p u (q e) -> p u q e", e=2),
                 banks["f", b, h, t][:].rearrange("p (q u e) -> p u q e", u=2, e=2))

        def turn(b, h, tt):
            bank = pst.tile([P, 2, 2, P], F32, name="tr")
            banks["t", b, h, tt] = bank
            for t2 in range(2):
                for u in range(2):
                    nc.tensor.transpose(bank[:, t2, u, :], f_sb[b, h][:, 2 * tt + t2, u, :].bitcast(F32), id_f[:])

        def turn_out(b, h, tt, eng):
            if tt == 0:
                t_g[b, h] = stage.tile([P, 2048], BF16, name="t_g", align_bytes=64)
            copy(eng, t_g[b, h][:, 1024 * tt : 1024 * (tt + 1)].bitcast(F32).rearrange("p (r t u) -> p r t u", t=2, u=2),
                 banks["t", b, h, tt][:].rearrange("p t u r -> p r t u"))

        def g_int(b, h):
            g_g[b, h] = stage.tile([P, 2048], BF16, name="g_g", align_bytes=64)
            for u in range(2):
                nc.vector.tensor_copy(
                    out=g_g[b, h][:].rearrange("p (q u e t) -> p q u t e", u=2, e=2, t=PACK)[:, :, u],
                    in_=f_sb[b, h][:, :, u, :].rearrange("p t (q e) -> p q t e", e=2),
                )

        def g_quant(b, h):
            g_q[b, h] = codes_tile("g_q%d%d" % (b, h))
            quant(g_q[b, h], g_g[b, h], E5M2)

        def t_quant(b, h):
            t_q[b, h] = codes_tile("t_q%d%d" % (b, h))
            quant(t_q[b, h], t_g[b, h], E5M2)

        def wv_turn(i0, g, ii):
            bank = pst.tile([P, 2, 2, P], F32, name="tr")
            banks["w", i0, g, ii] = bank
            for i2 in range(2):
                words = wv_raw[i0, ii][:, i2, :].bitcast(F32)
                for u in range(2):
                    nc.tensor.transpose(bank[:, i2, u, :], words[:, 256 * g + u : 256 * (g + 1) : 2], id_f[:])

        def wv_out(i0, g, ii, eng):
            if ii == 0:
                wv_g[i0, g] = stage.tile([P, 2048], BF16, name="wv_g", align_bytes=64)
            copy(eng, wv_g[i0, g][:, 1024 * ii : 1024 * (ii + 1)].bitcast(F32).rearrange("p (i r u) -> p i r u", i=2, u=2),
                 banks["w", i0, g, ii][:].rearrange("p i u r -> p i r u"))

        def wv_quant(i0, g):
            wv_q[i0, g] = codes_tile("wv_q%d%d" % (i0, g))
            quant(wv_q[i0, g], wv_g[i0, g], E4M3)

        def x_int(b, n, eng):
            x_g[b, n] = stage.tile([P, 2048], BF16, name="x_g", align_bytes=64, bufs=3)
            copy(eng, x_g[b, n][:].rearrange("p (c i j) -> p c j i", i=4, j=PACK),
                 x_raw[b][:, :, 512 * n : 512 * (n + 1)].rearrange("p j (c i) -> p c j i", i=4))

        def x_quant(b, n):
            x_q[b, n] = codes_tile("x_q%d%d" % (b, n))
            quant(x_q[b, n], x_g[b, n], E4M3)

        ots = {}

        def out0_mm(b, i, n, h):
            bank = mm_bank("o0", b, i, n) if h == 0 else banks["o0", b, i, n]
            mx(bank[:], g_q[b, h][0], g_q[b, h][1], E5M2, wv_q[n, h][0], wv_q[n, h][1], E4M3,
               slice(P * i, P * (i + 1)), slice(0, 512), h == 0, h == H - 1)

        def out0_ev(b, i, n, eng):
            if ("o0", b, i) not in ots:
                ot = outs.tile([P, D], F32, name="ot")
                ots["o0", b, i] = ot
            copy(eng, ots["o0", b, i][:, 512 * n : 512 * (n + 1)], banks["o0", b, i, n][:])

        def out0_st(b, i):
            nc.sync.dma_start(out=out_0[b, P * i : P * (i + 1), :], in_=ots["o0", b, i][:])

        def out1_mm(i, h, b):
            bank = mm_bank("o1", i, h) if b == 0 else banks["o1", i, h]
            mx(bank[:], x_q[b, i // 4][0], x_q[b, i // 4][1], E4M3, t_q[b, h][0], t_q[b, h][1], E5M2,
               slice(P * (i % 4), P * (i % 4 + 1)), slice(0, 512), b == 0, b == B - 1)

        def out1_ev(i, h, eng):
            if ("o1", i) not in ots:
                ot = outs.tile([P, E], F32, name="ot")
                ots["o1", i] = ot
            copy(eng, ots["o1", i][:, 512 * h : 512 * (h + 1)].rearrange("p (m t v) -> p m t v", t=2, v=2),
                 banks["o1", i, h][:].rearrange("p (t m v) -> p m t v", t=2, v=2))

        def out1_st(i):
            nc.sync.dma_start(out=out_1[P * i : P * (i + 1), :], in_=ots["o1", i][:])

        def out1_half(i, h):
            nc.sync.dma_start(out=out_1[P * i : P * (i + 1), 512 * h : 512 * (h + 1)], in_=ots["o1", i][:, 512 * h : 512 * (h + 1)])

        load_att(0, 0)
        load_w()
        consts(0)
        load_att2(0, 0)
        gf_pe(0, 0, 2)
        gf_lin()
        gf_pe(0, 0, 0)
        gf_pe(0, 0, 1)
        gf_sum(0, 0, 0)
        gf_sum(0, 0, 1)
        gf_sum(0, 0, 2)
        gf_pe(0, 0, 3)
        gf_sum(0, 0, 3)
        consts(1)
        load_do(0, 0)
        do_int(0, 0)
        load_wv(0, 0)
        wv_turn(0, 0, 0)
        wv_turn(0, 1, 0)
        load_att(0, 1)
        gf_pe(0, 1, 0)
        do_quant(0, 0)
        load_att2(0, 1)
        wv_out(0, 0, 0, 's')
        gf_pe(0, 1, 1)
        load_do(0, 1)
        gf_quant(0, 0)
        feat_mm(0, 0, 0)
        feat_mm(0, 0, 1)
        feat_mm(0, 0, 2)
        feat_out(0, 0, 0, 's')
        gf_pe(0, 1, 2)
        feat_out(0, 0, 1, 's')
        wv_out(0, 1, 0, 'v')
        do_int(0, 1)
        gf_sum(0, 1, 0)
        gf_sum(0, 1, 1)
        load_wv(0, 1)
        gf_pe(0, 1, 3)
        gf_sum(0, 1, 2)
        gf_sum(0, 1, 3)
        feat_out(0, 0, 2, 's')
        gf_quant(0, 1)
        wv_turn(0, 1, 1)
        wv_out(0, 1, 1, 's')
        do_quant(0, 1)
        wv_turn(0, 0, 1)
        feat_mm(0, 0, 3)
        feat_mm(0, 1, 0)
        wv_out(0, 0, 1, 's')
        feat_mm(0, 1, 1)
        feat_mm(0, 1, 2)
        load_att(1, 1)
        load_do_both(1)
        feat_out(0, 0, 3, 'v')
        feat_out(0, 1, 0, 'v')
        feat_out(0, 1, 1, 's')
        feat_out(0, 1, 2, 's')
        feat_mm(0, 1, 3)
        feat_out(0, 1, 3, 's')
        turn(0, 0, 0)
        load_att2(1, 1)
        turn(0, 1, 0)
        turn_out(0, 1, 0, 's')
        gf_pe(1, 1, 1)
        g_int(0, 0)
        gf_pe(1, 1, 0)
        gf_pe(1, 1, 3)
        wv_quant(0, 0)
        g_int(0, 1)
        turn_out(0, 0, 0, 's')
        load_wv(1, 0)
        gf_sum(1, 1, 0)
        gf_sum(1, 1, 1)
        gf_pe(1, 1, 2)
        load_att(1, 0)
        gf_pe(1, 0, 0)
        gf_sum(1, 1, 2)
        gf_sum(1, 1, 3)
        wv_turn(1, 1, 0)
        do_int(1, 1)
        gf_pe(1, 0, 1)
        wv_quant(0, 1)
        do_int(1, 0)
        turn(0, 0, 1)
        wv_out(1, 1, 0, 's')
        gf_quant(1, 1)
        gf_pe(1, 0, 2)
        do_quant(1, 1)
        feat_mm(1, 1, 0)
        feat_mm(1, 1, 1)
        feat_mm(1, 1, 2)
        turn_out(0, 0, 1, 's')
        load_wv(1, 1)
        g_quant(0, 1)
        feat_out(1, 1, 0, 's')
        feat_out(1, 1, 1, 's')
        wv_turn(1, 1, 1)
        g_quant(0, 0)
        feat_out(1, 1, 2, 's')
        load_att2(1, 0)
        gf_sum(1, 0, 0)
        load_x(1)
        gf_pe(1, 0, 3)
        gf_sum(1, 0, 1)
        gf_sum(1, 0, 2)
        gf_sum(1, 0, 3)
        wv_turn(1, 0, 0)
        wv_out(1, 1, 1, 's')
        wv_turn(1, 0, 1)
        wv_out(1, 0, 0, 'v')
        do_quant(1, 0)
        feat_mm(1, 1, 3)
        out0_mm(0, 2, 0, 0)
        out0_mm(0, 2, 0, 1)
        x_int(1, 1, 's')
        gf_quant(1, 0)
        turn(0, 1, 1)
        wv_out(1, 0, 1, 's')
        feat_mm(1, 0, 0)
        wv_quant(1, 1)
        turn_out(0, 1, 1, 'v')
        out0_ev(0, 2, 0, 's')
        feat_mm(1, 0, 1)
        feat_mm(1, 0, 2)
        turn(1, 1, 0)
        wv_quant(1, 0)
        feat_mm(1, 0, 3)
        t_quant(0, 1)
        out0_mm(0, 2, 1, 0)
        out0_mm(0, 0, 1, 0)
        feat_out(1, 1, 3, 's')
        feat_out(1, 0, 0, 's')
        feat_out(1, 0, 1, 's')
        out0_mm(0, 2, 1, 1)
        t_quant(0, 0)
        out0_mm(0, 3, 0, 0)
        feat_out(1, 0, 2, 's')
        feat_out(1, 0, 3, 's')
        out0_mm(0, 0, 0, 0)
        out0_mm(0, 0, 0, 1)
        load_x(0)
        out0_mm(0, 0, 1, 1)
        x_int(0, 1, 'v')
        out0_mm(0, 3, 1, 0)
        out0_ev(0, 2, 1, 's')
        out0_mm(0, 1, 1, 0)
        g_int(1, 0)
        turn_out(1, 1, 0, 's')
        g_int(1, 1)
        out0_mm(0, 3, 0, 1)
        out0_mm(0, 1, 1, 1)
        out0_mm(0, 1, 0, 0)
        out0_mm(0, 1, 0, 1)
        out0_ev(0, 0, 0, 's')
        out0_ev(0, 0, 1, 's')
        out0_ev(0, 1, 0, 'v')
        out0_ev(0, 3, 0, 's')
        turn(1, 1, 1)
        turn(1, 0, 0)
        turn(1, 0, 1)
        out0_mm(0, 3, 1, 1)
        g_quant(1, 0)
        out0_mm(1, 1, 0, 0)
        g_quant(1, 1)
        out0_mm(1, 1, 0, 1)
        out0_ev(0, 1, 1, 's')
        turn_out(1, 1, 1, 's')
        out0_mm(1, 3, 0, 0)
        out0_ev(0, 3, 1, 'v')
        x_int(1, 0, 's')
        x_quant(0, 1)
        out0_mm(1, 1, 1, 0)
        out0_mm(1, 1, 1, 1)
        out0_ev(1, 1, 0, 's')
        out0_ev(1, 1, 1, 's')
        out0_mm(1, 3, 0, 1)
        x_quant(1, 1)
        out1_mm(6, 1, 0)
        t_quant(1, 1)
        out1_mm(6, 0, 0)
        out1_mm(6, 1, 1)
        out0_st(0, 2)
        out0_st(0, 0)
        out0_mm(1, 3, 1, 0)
        out0_mm(1, 3, 1, 1)
        turn_out(1, 0, 0, 's')
        turn_out(1, 0, 1, 's')
        x_int(0, 0, 'v')
        out0_st(0, 1)
        out1_mm(4, 1, 0)
        out1_mm(4, 1, 1)
        out0_ev(1, 3, 0, 's')
        out0_ev(1, 3, 1, 's')
        out1_mm(4, 0, 0)
        t_quant(1, 0)
        out1_mm(6, 0, 1)
        out1_mm(4, 0, 1)
        x_quant(0, 0)
        out1_mm(1, 0, 0)
        out1_ev(6, 0, 'v')
        out1_mm(0, 0, 0)
        out1_mm(0, 1, 0)
        out1_ev(6, 1, 's')
        x_quant(1, 0)
        out1_ev(4, 0, 's')
        out1_ev(4, 1, 's')
        out0_st(0, 3)
        out0_st(1, 1)
        out1_mm(2, 0, 0)
        out1_mm(0, 0, 1)
        out1_ev(0, 0, 'v')
        out1_mm(0, 1, 1)
        out1_ev(0, 1, 'v')
        out0_st(1, 3)
        out1_mm(1, 0, 1)
        out1_mm(2, 0, 1)
        out1_mm(3, 0, 0)
        out1_mm(3, 0, 1)
        out1_mm(2, 1, 0)
        out1_mm(1, 1, 0)
        out1_mm(1, 1, 1)
        out1_mm(3, 1, 0)
        out1_ev(1, 0, 's')
        out1_st(6)
        out1_ev(2, 0, 'v')
        out1_mm(2, 1, 1)
        out1_st(4)
        out1_ev(2, 1, 'v')
        out1_ev(1, 1, 's')
        out1_st(0)
        out1_half(1, 0)
        out0_mm(1, 2, 0, 0)
        out1_half(1, 1)
        out1_ev(3, 0, 'v')
        out1_mm(5, 0, 0)
        out1_mm(5, 0, 1)
        out1_mm(3, 1, 1)
        out0_mm(1, 2, 0, 1)
        out1_ev(3, 1, 's')
        out1_st(2)
        out0_mm(1, 2, 1, 0)
        out0_mm(1, 2, 1, 1)
        out0_ev(1, 2, 0, 's')
        out0_mm(1, 0, 0, 0)
        out0_mm(1, 0, 0, 1)
        out0_ev(1, 0, 0, 's')
        out0_mm(1, 0, 1, 0)
        out0_mm(1, 0, 1, 1)
        out0_ev(1, 2, 1, 'v')
        out1_st(3)
        out0_st(1, 2)
        out1_mm(5, 1, 0)
        out0_ev(1, 0, 1, 'v')
        out1_mm(5, 1, 1)
        out1_ev(5, 0, 's')
        out0_st(1, 0)
        out1_ev(5, 1, 's')
        out1_mm(7, 1, 0)
        out1_st(5)
        out1_mm(7, 0, 0)
        out1_mm(7, 0, 1)
        out1_ev(7, 0, 'v')
        out1_mm(7, 1, 1)
        out1_ev(7, 1, 'v')
        out1_st(7)
